import numpy as np
import ml_dtypes


def mxq(x, axis, fmt="e4m3"):
    dtype, down = {"e4m3": (ml_dtypes.float8_e4m3fn, 7), "e5m2": (ml_dtypes.float8_e5m2, 14)}[fmt]
    v = np.moveaxis(np.asarray(x, np.float32).astype(ml_dtypes.bfloat16).astype(np.float64), axis, -1)
    blocks = v.reshape(v.shape[:-1] + (-1, 32))
    amax = np.abs(blocks).max(-1, keepdims=True)
    byte = np.maximum(np.where(amax > 0, np.frexp(amax)[1] - 1 + 127, 0) - down, 1)
    scale = np.exp2(byte - 127.0)
    codes = (blocks / scale).astype(np.float32).astype(dtype).astype(np.float64)
    return np.moveaxis((codes * scale).reshape(v.shape), -1, axis)


WIDE = False


def mx_kscale(k):
    if not WIDE:
        return np.ones(k)
    levels = np.array([10, -10, 5, -5, 0])
    a = np.random.permutation(np.resize(levels, k // 512 * 4)).reshape(k // 512, 4)
    idx = np.arange(k)
    return np.exp2(a[idx // 512, idx % 128 // 32])


BF16 = ml_dtypes.bfloat16


def bf(x):
    return np.asarray(x, np.float32).astype(BF16)


def f64(x):
    return np.asarray(x).astype(np.float64)


B, S, E, H, D, XL, TOPK = 1, 128, 128, 8, 128, 512, 8
HD = H * D
J = S * TOPK


def sigmoid(v):
    return 1.0 / (1.0 + np.exp(-v))


def setup_inputs():
    n = np.random.standard_normal
    t = mx_kscale(HD)
    k_ext = n((B, S, TOPK, HD)) * 1.5 * np.sqrt(HD)
    v_ext = (1.0 + 1.5 * n((B, S, TOPK, HD))) * t
    return {"q": bf(n((B, H, S, D)) / np.sqrt(HD)),
            "qkv": bf((0.25 + 0.5 * np.abs(n((B, H, S, D)))) * t.reshape(H, 1, D)),
            "kv_external": bf(np.stack([k_ext, v_ext], axis=-2)),
            "gate": bf(n((H, 1, 1))),
            "Wo": bf(n((E, HD)) / np.sqrt(HD) / t),
            "bo": bf(n(E) * 0.1)}


def reference(q, qkv, kv_external, gate, Wo, bo):
    kv = f64(kv_external)
    k_ext = kv[..., 0, :].reshape(B, S, TOPK, H, D).transpose(0, 3, 1, 2, 4).reshape(B, H, J, D)
    v_ext = kv[..., 1, :].reshape(B, S, TOPK, H, D).transpose(0, 3, 1, 2, 4).reshape(B, H, J, D)
    s = f64(q) @ k_ext.transpose(0, 1, 3, 2) * D ** -0.5
    e = np.exp(s - s.max(-1, keepdims=True))
    qkv_ext = (mxq(e, 3, "e4m3") @ mxq(v_ext, 2, "e4m3")) / e.sum(-1, keepdims=True)
    g = sigmoid(f64(gate))
    fused = f64(qkv) * g + qkv_ext * (1.0 - g)
    merged = fused.transpose(0, 2, 1, 3).reshape(B, S, HD)
    return (mxq(merged, 2, "e4m3") @ mxq(f64(Wo), 1, "e4m3").T) + f64(bo)

@@ -1,0 +1,278 @@
+from contextlib import ExitStack
+
+import concourse.mybir as mybir
+from concourse.masks import make_identity
+
+BF16 = mybir.dt.bfloat16
+F32 = mybir.dt.float32
+U32 = mybir.dt.uint32
+U8 = mybir.dt.uint8
+FP8X4 = mybir.dt.float8_e4m3fn_x4
+ACT = mybir.ActivationFunctionType
+ALU = mybir.AluOpType
+AX = mybir.AxisListType
+
+P = 128
+H = 8
+D = 128
+S = 128
+T = 8
+HD = H * D
+KEYS = S * T
+BANK = 512
+PASSES = 2
+PAIRS = H // 2
+PAIR_COLS = 2 * D
+SCALE = D ** -0.5
+
+FLOPS = 2 * H * S * KEYS * D * 2 + 2 * S * HD * P
+
+
+def tile_knnxlmultiheadsattention_pb_s_kernel(tc, q, qkv, kv_external, gate, Wo, bo, out):
+    nc = tc.nc
+    kv = kv_external.rearrange("b j t c n -> (b j) t c n")
+
+    with ExitStack() as ctx:
+        keep = ctx.enter_context(tc.tile_pool(name="keep", bufs=1))
+        work = ctx.enter_context(tc.tile_pool(name="work", bufs=3))
+        psum = ctx.enter_context(tc.psum_pool(name="psum", bufs=1))
+        ctx.enter_context(tc.manual_schedule())
+
+        zero = keep.tile([P, 1], F32)
+        nc.vector.memset(zero[:], 0.0)
+        one = keep.tile([P, 1], F32)
+        nc.scalar.activation(out=one[:], in_=zero[:], func=ACT.Exp)
+        ident_bf = keep.tile([P, P], BF16)
+        make_identity(nc, ident_bf[:])
+        ident_f32 = keep.tile([P, P], F32)
+        make_identity(nc, ident_f32[:])
+
+        k_sb = [keep.tile([P, T, PAIR_COLS], BF16, name="k_sb%d" % c) for c in range(PAIRS)]
+        v_sb = [keep.tile([P, T, PAIR_COLS], BF16, name="v_sb%d" % c) for c in range(PAIRS)]
+        q_sb = keep.tile([P, H, D], BF16)
+        gate_sb = keep.tile([P, H], BF16)
+        qkv_sb = keep.tile([P, H, D], BF16)
+        wo_sb = keep.tile([P, HD], BF16)
+        bo_sb = keep.tile([P, P], BF16)
+
+        def load_k(c):
+            nc.sync.dma_start(out=k_sb[c][:], in_=kv[:, :, 0, c * PAIR_COLS : (c + 1) * PAIR_COLS])
+
+        def load_v(c):
+            nc.sync.dma_start(out=v_sb[c][:], in_=kv[:, :, 1, c * PAIR_COLS : (c + 1) * PAIR_COLS])
+
+        nc.sync.dma_start(out=gate_sb[:], in_=gate.rearrange("h a b -> (h a b)").partition_broadcast(P))
+        load_k(0)
+        nc.sync.dma_start(out=q_sb[:], in_=q.rearrange("b h i d -> i (b h) d"))
+        load_k(1)
+        load_v(0)
+        nc.sync.dma_start(out=qkv_sb[:], in_=qkv.rearrange("b h i d -> i (b h) d"))
+        for c in range(2, PAIRS):
+            load_k(c)
+            load_v(c - 1)
+        load_v(PAIRS - 1)
+        nc.sync.dma_start(out=wo_sb[:], in_=Wo)
+        nc.sync.dma_start(out=bo_sb[:], in_=bo.partition_broadcast(P))
+
+        kT_ps, kT, s_ps, nb, e_sb, rs, eT_ps, eT_grp, e_codes, e_scales, cf, pv_ps = (
+            {}, {}, {}, {}, {}, {}, {}, {}, {}, {}, {}, {},
+        )
+        v_grp, v_codes, v_scales = {}, {}, {}
+        qT = keep.tile([P, H, S], BF16)
+        den = keep.tile([P, 2 * H], F32)
+        g_sb = keep.tile([P, H], F32)
+        qg = keep.tile([P, H, D], F32)
+        merged = keep.tile([P, HD], BF16)
+
+        def turn_words(turned, rows, first, count):
+            words = rows.bitcast(F32)
+            for b in range(count):
+                nc.tensor.transpose(turned[:, b, :], words[:, (first + b) * P : (first + b + 1) * P], ident_f32[:])
+
+        def regroup_words(copy, grouped, turned):
+            copy(
+                out=grouped.bitcast(F32).rearrange("p (g r u) -> p g r u", r=P, u=2),
+                in_=turned.rearrange("p (g u) r -> p g r u", u=2),
+            )
+
+        def turn_keys(h):
+            kT_ps[h] = psum.tile([P, T, P], BF16, name="kT_ps", tag="tp", bufs=2)
+            cols = slice((h % 2) * D, (h % 2 + 1) * D)
+            for t in range(T):
+                nc.tensor.transpose(kT_ps[h][:, t, :], k_sb[h // 2][:, t, cols], ident_bf[:])
+
+        def keep_keys(h):
+            kT[h] = keep.tile([P, KEYS], BF16, name="kT%d" % h)
+            nc.scalar.copy(out=kT[h][:], in_=kT_ps[h][:].rearrange("p t j -> p (t j)"))
+
+        def scores(h):
+            s_ps[h] = []
+            for g in range(PASSES):
+                s_g = psum.tile([P, BANK], F32, tag="s", bufs=4)
+                nc.tensor.matmul(
+                    s_g[:], lhsT=qT[:, h, :], rhs=kT[h][:, g * BANK : (g + 1) * BANK], start=True, stop=True
+                )
+                s_ps[h].append(s_g)
+
+        def row_max(h):
+            mx = work.tile([P, PASSES], F32, tag="mx")
+            for g in range(PASSES):
+                nc.vector.reduce_max(out=mx[:, g : g + 1], in_=s_ps[h][g][:], axis=AX.X)
+            nb[h] = work.tile([P, 1], F32, name="nb", tag="nb")
+            nc.vector.tensor_scalar(
+                out=nb[h][:], in0=mx[:, 0:1], scalar1=mx[:, 1:2], scalar2=-SCALE, op0=ALU.max, op1=ALU.mult
+            )
+
+        def exponentials(h):
+            e_sb[h] = work.tile([P, KEYS], BF16, name="e_sb", tag="e_sb")
+            rs[h] = work.tile([P, PASSES], F32, name="rs", tag="rs")
+            for g in range(PASSES):
+                nc.scalar.activation(
+                    out=e_sb[h][:, g * BANK : (g + 1) * BANK].rearrange("p (u j e) -> p u j e", u=2, e=2),
+                    in_=s_ps[h][g][:].rearrange("p (u e j) -> p u j e", u=2, e=2),
+                    func=ACT.Exp,
+                    bias=nb[h][:, 0:1],
+                    scale=SCALE,
+                    accum_out=rs[h][:, g : g + 1],
+                )
+
+        def turn_e(h):
+            eT_ps[h] = psum.tile([P, 2 * PASSES, P], F32, name="eT_ps", tag="turned", bufs=1)
+            turn_words(eT_ps[h], e_sb[h][:], 0, 2 * PASSES)
+
+        def keep_e(h):
+            eT_grp[h] = work.tile([P, KEYS], BF16, name="eT_grp", tag="eT_grp", align_bytes=64)
+            regroup_words(nc.scalar.copy, eT_grp[h][:], eT_ps[h][:])
+
+        def quantise_e(h):
+            e_codes[h] = work.tile([P, PASSES * P], U32, name="e_codes", tag="e_codes", align_bytes=64)
+            e_scales[h] = work.tile([P, PASSES * P], U8, name="e_scales", tag="e_scales", align_bytes=64)
+            nc.vector.quantize_mx(out=e_codes[h][:].bitcast(FP8X4), scales=e_scales[h][:], in_=eT_grp[h][:])
+            dn = work.tile([P, 1], F32, tag="dn")
+            nc.vector.tensor_scalar(
+                out=dn[:], in0=rs[h][:, 0:1], scalar1=rs[h][:, 1:2], scalar2=den[:, H + h : H + h + 1],
+                op0=ALU.add, op1=ALU.mult,
+            )
+            cf[h] = work.tile([P, 1], F32, name="cf", tag="cf")
+            nc.vector.reciprocal(out=cf[h][:], in_=dn[:])
+
+        def weighted_values(h):
+            pv_ps[h] = psum.tile([P, D], F32, name="pv_ps", tag="pv", bufs=1)
+            cols = slice((h % 2) * D, (h % 2 + 1) * D)
+            for g in range(PASSES):
+                nc.tensor.matmul_mx(
+                    out=pv_ps[h][:],
+                    lhsT=e_codes[h][:, g * P : (g + 1) * P].bitcast(FP8X4),
+                    lhsT_scale=e_scales[h][:, g * P : (g + 1) * P],
+                    rhs=v_codes[h // 2][:, g, cols].bitcast(FP8X4),
+                    rhs_scale=v_scales[h // 2][:, g, cols],
+                    start=(g == 0),
+                    stop=(g == PASSES - 1),
+                )
+
+        def fuse(h):
+            nc.vector.scalar_tensor_tensor(
+                out=merged[:, h * D : (h + 1) * D], in0=pv_ps[h][:], scalar=cf[h][:, 0:1], in1=qg[:, h, :],
+                op0=ALU.mult, op1=ALU.add,
+            )
+
+        def regroup_values(c, g):
+            if g == 0:
+                v_grp[c] = keep.tile([P, PASSES, PAIR_COLS, 4], BF16, name="v_grp%d" % c, align_bytes=64)
+            nc.vector.tensor_copy(
+                out=v_grp[c][:, g].rearrange("p (c i) t -> p c t i", i=4),
+                in_=v_sb[c][:, 4 * g : 4 * g + 4, :].rearrange("p t (c i) -> p c t i", i=4),
+            )
+
+        def quantise_values(c):
+            v_codes[c] = keep.tile([P, PASSES, PAIR_COLS], U32, name="v_codes%d" % c, align_bytes=64)
+            v_scales[c] = keep.tile([P, PASSES, PAIR_COLS], U8, name="v_scales%d" % c, align_bytes=64)
+            nc.vector.quantize_mx(
+                out=v_codes[c][:].rearrange("p g c -> p (g c)").bitcast(FP8X4),
+                scales=v_scales[c][:].rearrange("p g c -> p (g c)"),
+                in_=v_grp[c][:].rearrange("p g c t -> p (g c t)"),
+            )
+
+        def is_head(h):
+            return 0 <= h < H
+
+        nc.scalar.activation(out=den[:, 0:H], in_=gate_sb[:], func=ACT.Exp, scale=-1.0)
+        nc.scalar.activation(out=den[:, H : 2 * H], in_=gate_sb[:], func=ACT.Exp, scale=1.0)
+        nc.vector.tensor_scalar_add(out=den[:], in0=den[:], scalar1=1.0)
+        nc.vector.reciprocal(out=g_sb[:], in_=den[:, 0:H])
+        nc.gpsimd.tensor_tensor(
+            out=qg[:], in0=qkv_sb[:], in1=g_sb[:].unsqueeze(2).to_broadcast([P, H, D]), op=ALU.mult
+        )
+        turn_keys(0)
+        qT_ps = psum.tile([P, H, S], BF16, tag="tp", bufs=2)
+        for h in range(H):
+            nc.tensor.transpose(qT_ps[:, h, :], q_sb[:, h, :], ident_bf[:])
+        nc.vector.tensor_copy(out=qT[:], in_=qT_ps[:])
+
+        for i in range(-2, H):
+            if is_head(i + 3):
+                turn_keys(i + 3)
+            if is_head(i - 1):
+                quantise_e(i - 1)
+                weighted_values(i - 1)
+            if is_head(i):
+                exponentials(i)
+                turn_e(i)
+            if is_head(i + 2):
+                keep_keys(i + 2)
+                scores(i + 2)
+            if is_head(i):
+                keep_e(i)
+            if is_head(i + 1):
+                row_max(i + 1)
+            if is_head(i - 1):
+                fuse(i - 1)
+            if 0 <= i + 1 < H:
+                regroup_values((i + 1) // 2, (i + 1) % 2)
+                if (i + 1) % 2 == 1:
+                    quantise_values((i + 1) // 2)
+
+        w_ps = psum.tile([P, 2 * PASSES, P], F32, tag="tp", bufs=2)
+        turn_words(w_ps, wo_sb[:], 0, 2 * PASSES)
+        w_grp = keep.tile([P, HD], BF16, align_bytes=64)
+        regroup_words(nc.scalar.copy, w_grp[:], w_ps[:])
+        w_codes = keep.tile([P, PASSES * P], U32, align_bytes=64)
+        w_scales = keep.tile([P, PASSES * P], U8, align_bytes=64)
+
+        m_grp = [keep.tile([P, BANK], BF16, name="m_grp%d" % g, align_bytes=64) for g in range(PASSES)]
+        m_codes = [keep.tile([P, P], U32, name="m_codes%d" % g, align_bytes=64) for g in range(PASSES)]
+        m_scales = [keep.tile([P, P], U8, name="m_scales%d" % g, align_bytes=64) for g in range(PASSES)]
+        out_ps = psum.tile([P, P], F32, tag="s", bufs=4)
+
+        def quantise_merged(g):
+            nc.vector.quantize_mx(out=m_codes[g][:].bitcast(FP8X4), scales=m_scales[g][:], in_=m_grp[g][:])
+
+        def project(g):
+            nc.tensor.matmul_mx(
+                out=out_ps[:],
+                lhsT=m_codes[g][:].bitcast(FP8X4),
+                lhsT_scale=m_scales[g][:],
+                rhs=w_codes[:, g * P : (g + 1) * P].bitcast(FP8X4),
+                rhs_scale=w_scales[:, g * P : (g + 1) * P],
+                start=(g == 0),
+                stop=(g == PASSES - 1),
+            )
+
+        m0_ps = psum.tile([P, 2, P], F32, tag="tp", bufs=2)
+        turn_words(m0_ps, merged[:], 0, 2)
+        regroup_words(nc.scalar.copy, m_grp[0][:], m0_ps[:])
+
+        quantise_e(H - 1)
+        weighted_values(H - 1)
+        nc.vector.quantize_mx(out=w_codes[:].bitcast(FP8X4), scales=w_scales[:], in_=w_grp[:])
+        quantise_merged(0)
+        project(0)
+        fuse(H - 1)
+        m1_ps = psum.tile([P, 2, P], F32, tag="turned", bufs=1)
+        turn_words(m1_ps, merged[:], 2, 2)
+        regroup_words(nc.vector.tensor_copy, m_grp[1][:], m1_ps[:])
+        quantise_merged(1)
+        project(1)
+        out_sb = keep.tile([P, P], F32)
+        nc.vector.tensor_tensor(out=out_sb[:], in0=out_ps[:], in1=bo_sb[:], op=ALU.add)
+        nc.sync.dma_start(out=out.rearrange("b i e -> (b i) e"), in_=out_sb[:])

@@ -21,7 +21,7 @@ HD = H * D
 KEYS = S * T
 BANK = 512
 PASSES = 2
-PAIRS = H // 2
+PACK = 4
 PAIR_COLS = 2 * D
 SCALE = D ** -0.5
 
@@ -47,42 +47,45 @@ def tile_knnxlmultiheadsattention_pb_s_kernel(tc, q, qkv, kv_external, gate, Wo,
         ident_f32 = keep.tile([P, P], F32)
         make_identity(nc, ident_f32[:])
 
-        k_sb = [keep.tile([P, T, PAIR_COLS], BF16, name="k_sb%d" % c) for c in range(PAIRS)]
-        v_sb = [keep.tile([P, T, PAIR_COLS], BF16, name="v_sb%d" % c) for c in range(PAIRS)]
-        q_sb = keep.tile([P, H, D], BF16)
+        k_sb = [keep.tile([P, HD], BF16, name="k_sb%d" % t) for t in range(T)]
+        v_sb = [keep.tile([P, PACK, HD], BF16, name="v_sb%d" % g) for g in range(PASSES)]
+        q_sb = keep.tile([P, HD], BF16)
         gate_sb = keep.tile([P, H], BF16)
         qkv_sb = keep.tile([P, H, D], BF16)
         wo_sb = keep.tile([P, HD], BF16)
         bo_sb = keep.tile([P, P], BF16)
 
-        def load_k(c):
-            nc.sync.dma_start(out=k_sb[c][:], in_=kv[:, :, 0, c * PAIR_COLS : (c + 1) * PAIR_COLS])
-
-        def load_v(c):
-            nc.sync.dma_start(out=v_sb[c][:], in_=kv[:, :, 1, c * PAIR_COLS : (c + 1) * PAIR_COLS])
-
         nc.sync.dma_start(out=gate_sb[:], in_=gate.rearrange("h a b -> (h a b)").partition_broadcast(P))
-        load_k(0)
-        nc.sync.dma_start(out=q_sb[:], in_=q.rearrange("b h i d -> i (b h) d"))
-        load_k(1)
-        load_v(0)
+        nc.sync.dma_start(out=k_sb[0][:], in_=kv[:, 0, 0, :])
+        nc.sync.dma_start(
+            out=q_sb[:].rearrange("i (h d) -> i h d", h=H), in_=q.rearrange("b h i d -> i (b h) d")
+        )
+        for t in range(1, T):
+            nc.sync.dma_start(out=k_sb[t][:], in_=kv[:, t, 0, :])
+        nc.sync.dma_start(out=v_sb[0][:], in_=kv[:, 0:PACK, 1, :])
         nc.sync.dma_start(out=qkv_sb[:], in_=qkv.rearrange("b h i d -> i (b h) d"))
-        for c in range(2, PAIRS):
-            load_k(c)
-            load_v(c - 1)
-        load_v(PAIRS - 1)
+        nc.sync.dma_start(out=v_sb[1][:], in_=kv[:, PACK : 2 * PACK, 1, :])
         nc.sync.dma_start(out=wo_sb[:], in_=Wo)
         nc.sync.dma_start(out=bo_sb[:], in_=bo.partition_broadcast(P))
 
-        kT_ps, kT, s_ps, nb, e_sb, rs, eT_ps, eT_grp, e_codes, e_scales, cf, pv_ps = (
-            {}, {}, {}, {}, {}, {}, {}, {}, {}, {}, {}, {},
-        )
+        s_ps, nb, e_sb, rs, eT_ps, eT_grp, e_codes, e_scales, cf, pv_ps = {}, {}, {}, {}, {}, {}, {}, {}, {}, {}
         v_grp, v_codes, v_scales = {}, {}, {}
         qT = keep.tile([P, H, S], BF16)
+        kT = keep.tile([P, H, KEYS], BF16)
         den = keep.tile([P, 2 * H], F32)
         g_sb = keep.tile([P, H], F32)
         qg = keep.tile([P, H, D], F32)
         merged = keep.tile([P, HD], BF16)
+
+        def turn_heads(rows, turned_lo, turned_hi):
+            lo_ps = psum.tile([P, H // 2, P], BF16, tag="s", bufs=4)
+            hi_ps = psum.tile([P, H // 2, P], BF16, tag="s", bufs=4)
+            for h in range(H // 2):
+                nc.tensor.transpose(lo_ps[:, h, :], rows[:, h * D : (h + 1) * D], ident_bf[:])
+            for h in range(H // 2):
+                nc.tensor.transpose(hi_ps[:, h, :], rows[:, (H // 2 + h) * D : (H // 2 + h + 1) * D], ident_bf[:])
+            nc.vector.tensor_copy(out=turned_lo, in_=lo_ps[:])
+            nc.scalar.copy(out=turned_hi, in_=hi_ps[:])
 
         def turn_words(turned, rows, first, count):
             words = rows.bitcast(F32)
@@ -95,22 +98,12 @@ def tile_knnxlmultiheadsattention_pb_s_kernel(tc, q, qkv, kv_external, gate, Wo,
                 in_=turned.rearrange("p (g u) r -> p g r u", u=2),
             )
 
-        def turn_keys(h):
-            kT_ps[h] = psum.tile([P, T, P], BF16, name="kT_ps", tag="tp", bufs=2)
-            cols = slice((h % 2) * D, (h % 2 + 1) * D)
-            for t in range(T):
-                nc.tensor.transpose(kT_ps[h][:, t, :], k_sb[h // 2][:, t, cols], ident_bf[:])
-
-        def keep_keys(h):
-            kT[h] = keep.tile([P, KEYS], BF16, name="kT%d" % h)
-            nc.scalar.copy(out=kT[h][:], in_=kT_ps[h][:].rearrange("p t j -> p (t j)"))
-
         def scores(h):
             s_ps[h] = []
             for g in range(PASSES):
                 s_g = psum.tile([P, BANK], F32, tag="s", bufs=4)
                 nc.tensor.matmul(
-                    s_g[:], lhsT=qT[:, h, :], rhs=kT[h][:, g * BANK : (g + 1) * BANK], start=True, stop=True
+                    s_g[:], lhsT=qT[:, h, :], rhs=kT[:, h, g * BANK : (g + 1) * BANK], start=True, stop=True
                 )
                 s_ps[h].append(s_g)
 
@@ -137,7 +130,7 @@ def tile_knnxlmultiheadsattention_pb_s_kernel(tc, q, qkv, kv_external, gate, Wo,
                 )
 
         def turn_e(h):
-            eT_ps[h] = psum.tile([P, 2 * PASSES, P], F32, name="eT_ps", tag="turned", bufs=1)
+            eT_ps[h] = psum.tile([P, 2 * PASSES, P], F32, name="eT_ps", tag="turned", bufs=2)
             turn_words(eT_ps[h], e_sb[h][:], 0, 2 * PASSES)
 
         def keep_e(h):
@@ -157,7 +150,7 @@ def tile_knnxlmultiheadsattention_pb_s_kernel(tc, q, qkv, kv_external, gate, Wo,
             nc.vector.reciprocal(out=cf[h][:], in_=dn[:])
 
         def weighted_values(h):
-            pv_ps[h] = psum.tile([P, D], F32, name="pv_ps", tag="pv", bufs=1)
+            pv_ps[h] = psum.tile([P, D], F32, name="pv_ps", tag="pv", bufs=2)
             cols = slice((h % 2) * D, (h % 2 + 1) * D)
             for g in range(PASSES):
                 nc.tensor.matmul_mx(
@@ -178,10 +171,10 @@ def tile_knnxlmultiheadsattention_pb_s_kernel(tc, q, qkv, kv_external, gate, Wo,
 
         def regroup_values(c, g):
             if g == 0:
-                v_grp[c] = keep.tile([P, PASSES, PAIR_COLS, 4], BF16, name="v_grp%d" % c, align_bytes=64)
+                v_grp[c] = keep.tile([P, PASSES, PAIR_COLS, PACK], BF16, name="v_grp%d" % c, align_bytes=64)
             nc.vector.tensor_copy(
                 out=v_grp[c][:, g].rearrange("p (c i) t -> p c t i", i=4),
-                in_=v_sb[c][:, 4 * g : 4 * g + 4, :].rearrange("p t (c i) -> p c t i", i=4),
+                in_=v_sb[g][:, :, c * PAIR_COLS : (c + 1) * PAIR_COLS].rearrange("p t (c i) -> p c t i", i=4),
             )
 
         def quantise_values(c):
@@ -203,36 +196,34 @@ def tile_knnxlmultiheadsattention_pb_s_kernel(tc, q, qkv, kv_external, gate, Wo,
         nc.gpsimd.tensor_tensor(
             out=qg[:], in0=qkv_sb[:], in1=g_sb[:].unsqueeze(2).to_broadcast([P, H, D]), op=ALU.mult
         )
-        turn_keys(0)
-        qT_ps = psum.tile([P, H, S], BF16, tag="tp", bufs=2)
-        for h in range(H):
-            nc.tensor.transpose(qT_ps[:, h, :], q_sb[:, h, :], ident_bf[:])
-        nc.vector.tensor_copy(out=qT[:], in_=qT_ps[:])
 
-        for i in range(-2, H):
-            if is_head(i + 3):
-                turn_keys(i + 3)
+        turn_heads(k_sb[0][:], kT[:, 0 : H // 2, 0:P], kT[:, H // 2 : H, 0:P])
+        turn_heads(q_sb[:], qT[:, 0 : H // 2, :], qT[:, H // 2 : H, :])
+        for t in range(1, T):
+            turn_heads(k_sb[t][:], kT[:, 0 : H // 2, t * P : (t + 1) * P], kT[:, H // 2 : H, t * P : (t + 1) * P])
+
+        for i in range(-2, H + 1):
             if is_head(i - 1):
-                quantise_e(i - 1)
-                weighted_values(i - 1)
-            if is_head(i):
-                exponentials(i)
-                turn_e(i)
-            if is_head(i + 2):
-                keep_keys(i + 2)
-                scores(i + 2)
-            if is_head(i):
-                keep_e(i)
+                turn_e(i - 1)
             if is_head(i + 1):
                 row_max(i + 1)
+            if is_head(i - 2):
+                quantise_e(i - 2)
+                weighted_values(i - 2)
+            if is_head(i):
+                exponentials(i)
+            if is_head(i + 2):
+                scores(i + 2)
             if is_head(i - 1):
-                fuse(i - 1)
-            if 0 <= i + 1 < H:
-                regroup_values((i + 1) // 2, (i + 1) % 2)
-                if (i + 1) % 2 == 1:
-                    quantise_values((i + 1) // 2)
+                keep_e(i - 1)
+            if is_head(i):
+                regroup_values(i // 2, i % 2)
+                if i % 2 == 1:
+                    quantise_values(i // 2)
+            if is_head(i - 2):
+                fuse(i - 2)
 
-        w_ps = psum.tile([P, 2 * PASSES, P], F32, tag="tp", bufs=2)
+        w_ps = psum.tile([P, 2 * PASSES, P], F32, tag="s", bufs=4)
         turn_words(w_ps, wo_sb[:], 0, 2 * PASSES)
         w_grp = keep.tile([P, HD], BF16, align_bytes=64)
         regroup_words(nc.scalar.copy, w_grp[:], w_ps[:])
@@ -258,7 +249,7 @@ def tile_knnxlmultiheadsattention_pb_s_kernel(tc, q, qkv, kv_external, gate, Wo,
                 stop=(g == PASSES - 1),
             )
 
-        m0_ps = psum.tile([P, 2, P], F32, tag="tp", bufs=2)
+        m0_ps = psum.tile([P, 2, P], F32, tag="s", bufs=4)
         turn_words(m0_ps, merged[:], 0, 2)
         regroup_words(nc.scalar.copy, m_grp[0][:], m0_ps[:])
 
@@ -268,7 +259,7 @@ def tile_knnxlmultiheadsattention_pb_s_kernel(tc, q, qkv, kv_external, gate, Wo,
         quantise_merged(0)
         project(0)
         fuse(H - 1)
-        m1_ps = psum.tile([P, 2, P], F32, tag="turned", bufs=1)
+        m1_ps = psum.tile([P, 2, P], F32, tag="turned", bufs=2)
         turn_words(m1_ps, merged[:], 2, 2)
         regroup_words(nc.vector.tensor_copy, m_grp[1][:], m1_ps[:])
         quantise_merged(1)

@@ -68,7 +68,7 @@ def tile_knnxlmultiheadsattention_pb_s_kernel(tc, q, qkv, kv_external, gate, Wo,
         nc.sync.dma_start(out=wo_sb[:], in_=Wo)
         nc.sync.dma_start(out=bo_sb[:], in_=bo.partition_broadcast(P))
 
-        s_ps, nb, e_sb, rs, eT_ps, eT_grp, e_codes, e_scales, cf, pv_ps = {}, {}, {}, {}, {}, {}, {}, {}, {}, {}
+        s_ps, nb, e_sb, rs, dn, eT_ps, eT_grp, e_codes, e_scales, cf, pv_ps = {}, {}, {}, {}, {}, {}, {}, {}, {}, {}, {}
         v_grp, v_codes, v_scales = {}, {}, {}
         qT = keep.tile([P, H, S], BF16)
         kT = keep.tile([P, H, KEYS], BF16)
@@ -112,7 +112,7 @@ def tile_knnxlmultiheadsattention_pb_s_kernel(tc, q, qkv, kv_external, gate, Wo,
             for g in range(PASSES):
                 nc.vector.reduce_max(out=mx[:, g : g + 1], in_=s_ps[h][g][:], axis=AX.X)
             nb[h] = work.tile([P, 1], F32, name="nb", tag="nb")
-            nc.vector.tensor_scalar(
+            nc.gpsimd.tensor_scalar(
                 out=nb[h][:], in0=mx[:, 0:1], scalar1=mx[:, 1:2], scalar2=-SCALE, op0=ALU.max, op1=ALU.mult
             )
 
@@ -128,6 +128,17 @@ def tile_knnxlmultiheadsattention_pb_s_kernel(tc, q, qkv, kv_external, gate, Wo,
                     scale=SCALE,
                     accum_out=rs[h][:, g : g + 1],
                 )
+            dn[h] = work.tile([P, 1], F32, name="dn", tag="dn")
+            nc.gpsimd.tensor_scalar(
+                out=dn[h][:], in0=rs[h][:, 0:1], scalar1=rs[h][:, 1:2], scalar2=den[:, H + h : H + h + 1],
+                op0=ALU.add, op1=ALU.mult,
+            )
+
+        def gate_local(h):
+            nc.gpsimd.tensor_scalar(
+                out=qg[:, h, :], in0=qkv_sb[:, h, :], scalar1=g_sb[:, h : h + 1], scalar2=0.0,
+                op0=ALU.mult, op1=ALU.add,
+            )
 
         def turn_e(h):
             eT_ps[h] = psum.tile([P, 2 * PASSES, P], F32, name="eT_ps", tag="turned", bufs=2)
@@ -141,13 +152,10 @@ def tile_knnxlmultiheadsattention_pb_s_kernel(tc, q, qkv, kv_external, gate, Wo,
             e_codes[h] = work.tile([P, PASSES * P], U32, name="e_codes", tag="e_codes", align_bytes=64)
             e_scales[h] = work.tile([P, PASSES * P], U8, name="e_scales", tag="e_scales", align_bytes=64)
             nc.vector.quantize_mx(out=e_codes[h][:].bitcast(FP8X4), scales=e_scales[h][:], in_=eT_grp[h][:])
-            dn = work.tile([P, 1], F32, tag="dn")
-            nc.vector.tensor_scalar(
-                out=dn[:], in0=rs[h][:, 0:1], scalar1=rs[h][:, 1:2], scalar2=den[:, H + h : H + h + 1],
-                op0=ALU.add, op1=ALU.mult,
-            )
+
+        def invert_sum(h):
             cf[h] = work.tile([P, 1], F32, name="cf", tag="cf")
-            nc.vector.reciprocal(out=cf[h][:], in_=dn[:])
+            nc.vector.reciprocal(out=cf[h][:], in_=dn[h][:])
 
         def weighted_values(h):
             pv_ps[h] = psum.tile([P, D], F32, name="pv_ps", tag="pv", bufs=2)
@@ -169,10 +177,10 @@ def tile_knnxlmultiheadsattention_pb_s_kernel(tc, q, qkv, kv_external, gate, Wo,
                 op0=ALU.mult, op1=ALU.add,
             )
 
-        def regroup_values(c, g):
+        def regroup_values(copy, c, g):
             if g == 0:
                 v_grp[c] = keep.tile([P, PASSES, PAIR_COLS, PACK], BF16, name="v_grp%d" % c, align_bytes=64)
-            nc.vector.tensor_copy(
+            copy(
                 out=v_grp[c][:, g].rearrange("p (c i) t -> p c t i", i=4),
                 in_=v_sb[g][:, :, c * PAIR_COLS : (c + 1) * PAIR_COLS].rearrange("p t (c i) -> p c t i", i=4),
             )
@@ -193,9 +201,6 @@ def tile_knnxlmultiheadsattention_pb_s_kernel(tc, q, qkv, kv_external, gate, Wo,
         nc.scalar.activation(out=den[:, H : 2 * H], in_=gate_sb[:], func=ACT.Exp, scale=1.0)
         nc.vector.tensor_scalar_add(out=den[:], in0=den[:], scalar1=1.0)
         nc.vector.reciprocal(out=g_sb[:], in_=den[:, 0:H])
-        nc.gpsimd.tensor_tensor(
-            out=qg[:], in0=qkv_sb[:], in1=g_sb[:].unsqueeze(2).to_broadcast([P, H, D]), op=ALU.mult
-        )
 
         turn_heads(k_sb[0][:], kT[:, 0 : H // 2, 0:P], kT[:, H // 2 : H, 0:P])
         turn_heads(q_sb[:], qT[:, 0 : H // 2, :], qT[:, H // 2 : H, :])
@@ -212,14 +217,18 @@ def tile_knnxlmultiheadsattention_pb_s_kernel(tc, q, qkv, kv_external, gate, Wo,
                 weighted_values(i - 2)
             if is_head(i):
                 exponentials(i)
+                gate_local(i)
             if is_head(i + 2):
                 scores(i + 2)
             if is_head(i - 1):
                 keep_e(i - 1)
-            if is_head(i):
-                regroup_values(i // 2, i % 2)
-                if i % 2 == 1:
-                    quantise_values(i // 2)
+            if is_head(i - 1):
+                invert_sum(i - 1)
+            if is_head(i) and i % 2 == 0:
+                regroup_values(nc.scalar.copy, i // 2, 0)
+            if is_head(i) and i % 2 == 1:
+                regroup_values(nc.vector.tensor_copy, i // 2, 1)
+                quantise_values(i // 2)
             if is_head(i - 2):
                 fuse(i - 2)
 

@@ -23,6 +23,8 @@ BANK = 512
 PASSES = 2
 PACK = 4
 PAIR_COLS = 2 * D
+HALF = H // 2
+HALF_COLS = HALF * D
 SCALE = D ** -0.5
 
 FLOPS = 2 * H * S * KEYS * D * 2 + 2 * S * HD * P
@@ -31,6 +33,7 @@ FLOPS = 2 * H * S * KEYS * D * 2 + 2 * S * HD * P
 def tile_knnxlmultiheadsattention_pb_s_kernel(tc, q, qkv, kv_external, gate, Wo, bo, out):
     nc = tc.nc
     kv = kv_external.rearrange("b j t c n -> (b j) t c n")
+    q_rows = q.rearrange("b h i d -> i (b h) d")
 
     with ExitStack() as ctx:
         keep = ctx.enter_context(tc.tile_pool(name="keep", bufs=1))
@@ -47,28 +50,40 @@ def tile_knnxlmultiheadsattention_pb_s_kernel(tc, q, qkv, kv_external, gate, Wo,
         ident_f32 = keep.tile([P, P], F32)
         make_identity(nc, ident_f32[:])
 
-        k_sb = [keep.tile([P, HD], BF16, name="k_sb%d" % t) for t in range(T)]
-        v_sb = [keep.tile([P, PACK, HD], BF16, name="v_sb%d" % g) for g in range(PASSES)]
-        q_sb = keep.tile([P, HD], BF16)
+        k0_sb = [keep.tile([P, 2, PAIR_COLS], BF16, name="k0_sb%d" % w) for w in range(T // 2)]
+        k1_sb = keep.tile([P, T, PAIR_COLS], BF16)
+        kb_sb = [keep.tile([P, PACK, HALF_COLS], BF16, name="kb_sb%d" % g) for g in range(PASSES)]
+        v_sb = [
+            [keep.tile([P, PACK, HALF_COLS], BF16, name="v_sb%d%d" % (f, g)) for g in range(PASSES)] for f in range(2)
+        ]
+        q_sb = keep.tile([P, H, D], BF16)
         gate_sb = keep.tile([P, H], BF16)
         qkv_sb = keep.tile([P, H, D], BF16)
         wo_sb = keep.tile([P, HD], BF16)
         bo_sb = keep.tile([P, P], BF16)
+        half_cols = [slice(f * HALF_COLS, (f + 1) * HALF_COLS) for f in range(2)]
+        pass_ts = [slice(g * PACK, (g + 1) * PACK) for g in range(PASSES)]
 
+        for w in range(T // 2):
+            nc.sync.dma_start(out=k0_sb[w][:], in_=kv[:, 2 * w : 2 * w + 2, 0, 0:PAIR_COLS])
+            if w == 0:
+                nc.sync.dma_start(out=q_sb[:, 0:2, :], in_=q_rows[:, 0:2, :])
+        nc.sync.dma_start(out=k1_sb[:], in_=kv[:, :, 0, PAIR_COLS : 2 * PAIR_COLS])
+        nc.sync.dma_start(out=q_sb[:, 2:H, :], in_=q_rows[:, 2:H, :])
         nc.sync.dma_start(out=gate_sb[:], in_=gate.rearrange("h a b -> (h a b)").partition_broadcast(P))
-        nc.sync.dma_start(out=k_sb[0][:], in_=kv[:, 0, 0, :])
-        nc.sync.dma_start(
-            out=q_sb[:].rearrange("i (h d) -> i h d", h=H), in_=q.rearrange("b h i d -> i (b h) d")
-        )
-        for t in range(1, T):
-            nc.sync.dma_start(out=k_sb[t][:], in_=kv[:, t, 0, :])
-        nc.sync.dma_start(out=v_sb[0][:], in_=kv[:, 0:PACK, 1, :])
+        for g in range(PASSES):
+            nc.sync.dma_start(out=v_sb[0][g][:], in_=kv[:, pass_ts[g], 1, half_cols[0]])
+        for g in range(PASSES):
+            nc.sync.dma_start(out=kb_sb[g][:], in_=kv[:, pass_ts[g], 0, half_cols[1]])
         nc.sync.dma_start(out=qkv_sb[:], in_=qkv.rearrange("b h i d -> i (b h) d"))
-        nc.sync.dma_start(out=v_sb[1][:], in_=kv[:, PACK : 2 * PACK, 1, :])
+        for g in range(PASSES):
+            nc.sync.dma_start(out=v_sb[1][g][:], in_=kv[:, pass_ts[g], 1, half_cols[1]])
         nc.sync.dma_start(out=wo_sb[:], in_=Wo)
         nc.sync.dma_start(out=bo_sb[:], in_=bo.partition_broadcast(P))
 
-        s_ps, nb, e_sb, rs, dn, eT_ps, eT_grp, e_codes, e_scales, cf, pv_ps = {}, {}, {}, {}, {}, {}, {}, {}, {}, {}, {}
+        s_ps, nb, e_sb, rs, dn, eT_ps, eT_grp, e_codes, e_scales, cf, pv_ps, kT_ps = (
+            {}, {}, {}, {}, {}, {}, {}, {}, {}, {}, {}, {}
+        )
         v_grp, v_codes, v_scales = {}, {}, {}
         qT = keep.tile([P, H, S], BF16)
         kT = keep.tile([P, H, KEYS], BF16)
@@ -77,15 +92,33 @@ def tile_knnxlmultiheadsattention_pb_s_kernel(tc, q, qkv, kv_external, gate, Wo,
         qg = keep.tile([P, H, D], F32)
         merged = keep.tile([P, HD], BF16)
 
-        def turn_heads(rows, turned_lo, turned_hi):
-            lo_ps = psum.tile([P, H // 2, P], BF16, tag="s", bufs=4)
-            hi_ps = psum.tile([P, H // 2, P], BF16, tag="s", bufs=4)
-            for h in range(H // 2):
-                nc.tensor.transpose(lo_ps[:, h, :], rows[:, h * D : (h + 1) * D], ident_bf[:])
-            for h in range(H // 2):
-                nc.tensor.transpose(hi_ps[:, h, :], rows[:, (H // 2 + h) * D : (H // 2 + h + 1) * D], ident_bf[:])
-            nc.vector.tensor_copy(out=turned_lo, in_=lo_ps[:])
-            nc.scalar.copy(out=turned_hi, in_=hi_ps[:])
+        def turn_q(copy, lo, hi):
+            q_ps = psum.tile([P, H, P], BF16, tag="turned", bufs=3)
+            for h in range(lo, hi):
+                nc.tensor.transpose(q_ps[:, h, :], q_sb[:, h, :], ident_bf[:])
+            copy(out=qT[:, lo:hi, :], in_=q_ps[:, lo:hi, :])
+
+        def turn_first_keys(copy, w):
+            k_ps = psum.tile([P, 2, 2, P], BF16, tag="turned", bufs=3)
+            for h in range(2):
+                for t in range(2):
+                    nc.tensor.transpose(k_ps[:, h, t, :], k0_sb[w][:, t, h * D : (h + 1) * D], ident_bf[:])
+            copy(
+                out=kT[:, 0:2, 2 * w * P : (2 * w + 2) * P],
+                in_=k_ps[:].rearrange("p h t r -> p h (t r)"),
+            )
+
+        def turn_keys(h):
+            kT_ps[h] = psum.tile([P, T, P], BF16, name="kT_ps", tag="turned", bufs=3)
+            for t in range(T):
+                if h < HALF:
+                    rows = k1_sb[:, t, (h - 2) * D : (h - 1) * D]
+                else:
+                    rows = kb_sb[t // PACK][:, t % PACK, (h - HALF) * D : (h - HALF + 1) * D]
+                nc.tensor.transpose(kT_ps[h][:, t, :], rows, ident_bf[:])
+
+        def keep_keys(h):
+            nc.scalar.copy(out=kT[:, h, :], in_=kT_ps[h][:].rearrange("p t r -> p (t r)"))
 
         def turn_words(turned, rows, first, count):
             words = rows.bitcast(F32)
@@ -116,18 +149,20 @@ def tile_knnxlmultiheadsattention_pb_s_kernel(tc, q, qkv, kv_external, gate, Wo,
                 out=nb[h][:], in0=mx[:, 0:1], scalar1=mx[:, 1:2], scalar2=-SCALE, op0=ALU.max, op1=ALU.mult
             )
 
-        def exponentials(h):
-            e_sb[h] = work.tile([P, KEYS], BF16, name="e_sb", tag="e_sb")
-            rs[h] = work.tile([P, PASSES], F32, name="rs", tag="rs")
-            for g in range(PASSES):
-                nc.scalar.activation(
-                    out=e_sb[h][:, g * BANK : (g + 1) * BANK].rearrange("p (u j e) -> p u j e", u=2, e=2),
-                    in_=s_ps[h][g][:].rearrange("p (u e j) -> p u j e", u=2, e=2),
-                    func=ACT.Exp,
-                    bias=nb[h][:, 0:1],
-                    scale=SCALE,
-                    accum_out=rs[h][:, g : g + 1],
-                )
+        def exponentials(h, g):
+            if g == 0:
+                e_sb[h] = work.tile([P, KEYS], BF16, name="e_sb", tag="e_sb")
+                rs[h] = work.tile([P, PASSES], F32, name="rs", tag="rs")
+            nc.scalar.activation(
+                out=e_sb[h][:, g * BANK : (g + 1) * BANK].rearrange("p (u j e) -> p u j e", u=2, e=2),
+                in_=s_ps[h][g][:].rearrange("p (u e j) -> p u j e", u=2, e=2),
+                func=ACT.Exp,
+                bias=nb[h][:, 0:1],
+                scale=SCALE,
+                accum_out=rs[h][:, g : g + 1],
+            )
+
+        def scale_sum(h):
             dn[h] = work.tile([P, 1], F32, name="dn", tag="dn")
             nc.gpsimd.tensor_scalar(
                 out=dn[h][:], in0=rs[h][:, 0:1], scalar1=rs[h][:, 1:2], scalar2=den[:, H + h : H + h + 1],
@@ -141,7 +176,7 @@ def tile_knnxlmultiheadsattention_pb_s_kernel(tc, q, qkv, kv_external, gate, Wo,
             )
 
         def turn_e(h):
-            eT_ps[h] = psum.tile([P, 2 * PASSES, P], F32, name="eT_ps", tag="turned", bufs=2)
+            eT_ps[h] = psum.tile([P, 2 * PASSES, P], F32, name="eT_ps", tag="turned", bufs=3)
             turn_words(eT_ps[h], e_sb[h][:], 0, 2 * PASSES)
 
         def keep_e(h):
@@ -158,15 +193,15 @@ def tile_knnxlmultiheadsattention_pb_s_kernel(tc, q, qkv, kv_external, gate, Wo,
             nc.vector.reciprocal(out=cf[h][:], in_=dn[h][:])
 
         def weighted_values(h):
-            pv_ps[h] = psum.tile([P, D], F32, name="pv_ps", tag="pv", bufs=2)
+            pv_ps[h] = psum.tile([P, D], F32, name="pv_ps", tag="pv", bufs=1)
             cols = slice((h % 2) * D, (h % 2 + 1) * D)
             for g in range(PASSES):
                 nc.tensor.matmul_mx(
                     out=pv_ps[h][:],
                     lhsT=e_codes[h][:, g * P : (g + 1) * P].bitcast(FP8X4),
                     lhsT_scale=e_scales[h][:, g * P : (g + 1) * P],
-                    rhs=v_codes[h // 2][:, g, cols].bitcast(FP8X4),
-                    rhs_scale=v_scales[h // 2][:, g, cols],
+                    rhs=v_codes[h // 2, g][:, cols].bitcast(FP8X4),
+                    rhs_scale=v_scales[h // 2, g][:, cols],
                     start=(g == 0),
                     stop=(g == PASSES - 1),
                 )
@@ -178,74 +213,96 @@ def tile_knnxlmultiheadsattention_pb_s_kernel(tc, q, qkv, kv_external, gate, Wo,
             )
 
         def regroup_values(copy, c, g):
-            if g == 0:
-                v_grp[c] = keep.tile([P, PASSES, PAIR_COLS, PACK], BF16, name="v_grp%d" % c, align_bytes=64)
+            v_grp[c, g] = keep.tile([P, PAIR_COLS, PACK], BF16, name="v_grp%d%d" % (c, g), align_bytes=64)
+            cols = slice((c % 2) * PAIR_COLS, (c % 2 + 1) * PAIR_COLS)
             copy(
-                out=v_grp[c][:, g].rearrange("p (c i) t -> p c t i", i=4),
-                in_=v_sb[g][:, :, c * PAIR_COLS : (c + 1) * PAIR_COLS].rearrange("p t (c i) -> p c t i", i=4),
+                out=v_grp[c, g][:].rearrange("p (c i) t -> p c t i", i=4),
+                in_=v_sb[c // 2][g][:, :, cols].rearrange("p t (c i) -> p c t i", i=4),
             )
 
-        def quantise_values(c):
-            v_codes[c] = keep.tile([P, PASSES, PAIR_COLS], U32, name="v_codes%d" % c, align_bytes=64)
-            v_scales[c] = keep.tile([P, PASSES, PAIR_COLS], U8, name="v_scales%d" % c, align_bytes=64)
+        def quantise_values(c, g):
+            v_codes[c, g] = keep.tile([P, PAIR_COLS], U32, name="v_codes%d%d" % (c, g), align_bytes=64)
+            v_scales[c, g] = keep.tile([P, PAIR_COLS], U8, name="v_scales%d%d" % (c, g), align_bytes=64)
             nc.vector.quantize_mx(
-                out=v_codes[c][:].rearrange("p g c -> p (g c)").bitcast(FP8X4),
-                scales=v_scales[c][:].rearrange("p g c -> p (g c)"),
-                in_=v_grp[c][:].rearrange("p g c t -> p (g c t)"),
+                out=v_codes[c, g][:].bitcast(FP8X4),
+                scales=v_scales[c, g][:],
+                in_=v_grp[c, g][:].rearrange("p c t -> p (c t)"),
             )
 
         def is_head(h):
             return 0 <= h < H
 
-        nc.scalar.activation(out=den[:, 0:H], in_=gate_sb[:], func=ACT.Exp, scale=-1.0)
-        nc.scalar.activation(out=den[:, H : 2 * H], in_=gate_sb[:], func=ACT.Exp, scale=1.0)
-        nc.vector.tensor_scalar_add(out=den[:], in0=den[:], scalar1=1.0)
-        nc.vector.reciprocal(out=g_sb[:], in_=den[:, 0:H])
+        turn_first_keys(nc.vector.tensor_copy, 0)
+        turn_q(nc.scalar.copy, 0, 2)
+        turn_first_keys(nc.scalar.copy, 1)
+        turn_first_keys(nc.vector.tensor_copy, 2)
+        turn_first_keys(nc.scalar.copy, 3)
+        scores(0)
+        row_max(0)
+        scores(1)
+        turn_keys(2)
+        keep_keys(2)
+        turn_q(nc.scalar.copy, 2, H)
+        turn_keys(3)
 
-        turn_heads(k_sb[0][:], kT[:, 0 : H // 2, 0:P], kT[:, H // 2 : H, 0:P])
-        turn_heads(q_sb[:], qT[:, 0 : H // 2, :], qT[:, H // 2 : H, :])
-        for t in range(1, T):
-            turn_heads(k_sb[t][:], kT[:, 0 : H // 2, t * P : (t + 1) * P], kT[:, H // 2 : H, t * P : (t + 1) * P])
-
-        for i in range(-2, H + 1):
-            if is_head(i - 1):
-                turn_e(i - 1)
-            if is_head(i + 1):
-                row_max(i + 1)
-            if is_head(i - 2):
-                quantise_e(i - 2)
-                weighted_values(i - 2)
-            if is_head(i):
-                exponentials(i)
-                gate_local(i)
-            if is_head(i + 2):
-                scores(i + 2)
-            if is_head(i - 1):
-                keep_e(i - 1)
-            if is_head(i - 1):
-                invert_sum(i - 1)
-            if is_head(i) and i % 2 == 0:
-                regroup_values(nc.scalar.copy, i // 2, 0)
-            if is_head(i) and i % 2 == 1:
-                regroup_values(nc.vector.tensor_copy, i // 2, 1)
-                quantise_values(i // 2)
-            if is_head(i - 2):
-                fuse(i - 2)
-
-        w_ps = psum.tile([P, 2 * PASSES, P], F32, tag="s", bufs=4)
-        turn_words(w_ps, wo_sb[:], 0, 2 * PASSES)
-        w_grp = keep.tile([P, HD], BF16, align_bytes=64)
-        regroup_words(nc.scalar.copy, w_grp[:], w_ps[:])
-        w_codes = keep.tile([P, PASSES * P], U32, align_bytes=64)
-        w_scales = keep.tile([P, PASSES * P], U8, align_bytes=64)
-
-        m_grp = [keep.tile([P, BANK], BF16, name="m_grp%d" % g, align_bytes=64) for g in range(PASSES)]
-        m_codes = [keep.tile([P, P], U32, name="m_codes%d" % g, align_bytes=64) for g in range(PASSES)]
-        m_scales = [keep.tile([P, P], U8, name="m_scales%d" % g, align_bytes=64) for g in range(PASSES)]
-        out_ps = psum.tile([P, P], F32, tag="s", bufs=4)
-
-        def quantise_merged(g):
-            nc.vector.quantize_mx(out=m_codes[g][:].bitcast(FP8X4), scales=m_scales[g][:], in_=m_grp[g][:])
+        for r in range(H):
+            if is_head(r + 1):
+                row_max(r + 1)
+            if is_head(r - 2):
+                fuse(r - 2)
+            exponentials(r, 0)
+            exponentials(r, 1)
+            if is_head(r + 2):
+                scores(r + 2)
+            turn_e(r)
+            if is_head(r - 1):
+                keep_e(r - 1)
+            if is_head(r + 3):
+                keep_keys(r + 3)
+            if r == 5:
+                w_grp = keep.tile([P, HD], BF16, align_bytes=64)
+                regroup_words(nc.scalar.copy, w_grp[:], w_ps[:])
+                m_grp = [keep.tile([P, BANK], BF16, name="m_grp%d" % g, align_bytes=64) for g in range(PASSES)]
+                m_codes = [keep.tile([P, P], U32, name="m_codes%d" % g, align_bytes=64) for g in range(PASSES)]
+                m_scales = [keep.tile([P, P], U8, name="m_scales%d" % g, align_bytes=64) for g in range(PASSES)]
+            if r == 7:
+                regroup_words(nc.scalar.copy, m_grp[0][:], m0_ps[:])
+            c = (r + 1) // 2
+            if r == 0:
+                nc.scalar.activation(out=den[:, 0:H], in_=gate_sb[:], func=ACT.Exp, scale=-1.0)
+                nc.scalar.activation(out=den[:, H : 2 * H], in_=gate_sb[:], func=ACT.Exp, scale=1.0)
+                regroup_values(nc.vector.tensor_copy, 0, 0)
+                regroup_values(nc.vector.tensor_copy, 0, 1)
+                nc.vector.tensor_scalar_add(out=den[:], in0=den[:], scalar1=1.0)
+                quantise_values(0, 0)
+                nc.vector.reciprocal(out=g_sb[:], in_=den[:, 0:H])
+                quantise_values(0, 1)
+            elif r % 2 == 1:
+                if c < H // 2:
+                    regroup_values(nc.vector.tensor_copy, c, 0)
+            else:
+                regroup_values(nc.vector.tensor_copy, c, 1)
+                quantise_values(c, 0)
+            if is_head(r - 1):
+                scale_sum(r - 1)
+                gate_local(r - 1)
+                invert_sum(r - 1)
+                quantise_e(r - 1)
+                weighted_values(r - 1)
+            if r > 0 and r % 2 == 0:
+                quantise_values(c, 1)
+            if r == 6:
+                w_codes = keep.tile([P, PASSES * P], U32, align_bytes=64)
+                w_scales = keep.tile([P, PASSES * P], U8, align_bytes=64)
+                nc.vector.quantize_mx(out=w_codes[:].bitcast(FP8X4), scales=w_scales[:], in_=w_grp[:])
+            if is_head(r + 4):
+                turn_keys(r + 4)
+            if r == 4:
+                w_ps = psum.tile([P, 2 * PASSES, P], F32, tag="turned", bufs=3)
+                turn_words(w_ps, wo_sb[:], 0, 2 * PASSES)
+            if r == 6:
+                m0_ps = psum.tile([P, 2, P], F32, tag="turned", bufs=3)
+                turn_words(m0_ps, merged[:], 0, 2)
 
         def project(g):
             nc.tensor.matmul_mx(
@@ -258,20 +315,22 @@ def tile_knnxlmultiheadsattention_pb_s_kernel(tc, q, qkv, kv_external, gate, Wo,
                 stop=(g == PASSES - 1),
             )
 
-        m0_ps = psum.tile([P, 2, P], F32, tag="s", bufs=4)
-        turn_words(m0_ps, merged[:], 0, 2)
-        regroup_words(nc.scalar.copy, m_grp[0][:], m0_ps[:])
-
-        quantise_e(H - 1)
-        weighted_values(H - 1)
-        nc.vector.quantize_mx(out=w_codes[:].bitcast(FP8X4), scales=w_scales[:], in_=w_grp[:])
-        quantise_merged(0)
+        last = H - 1
+        keep_e(last)
+        nc.vector.quantize_mx(out=m_codes[0][:].bitcast(FP8X4), scales=m_scales[0][:], in_=m_grp[0][:])
+        fuse(last - 1)
+        scale_sum(last)
+        gate_local(last)
+        invert_sum(last)
+        quantise_e(last)
+        weighted_values(last)
+        out_ps = psum.tile([P, P], F32, tag="s", bufs=4)
         project(0)
-        fuse(H - 1)
-        m1_ps = psum.tile([P, 2, P], F32, tag="turned", bufs=2)
+        fuse(last)
+        m1_ps = psum.tile([P, 2, P], F32, tag="turned", bufs=3)
         turn_words(m1_ps, merged[:], 2, 2)
         regroup_words(nc.vector.tensor_copy, m_grp[1][:], m1_ps[:])
-        quantise_merged(1)
+        nc.vector.quantize_mx(out=m_codes[1][:].bitcast(FP8X4), scales=m_scales[1][:], in_=m_grp[1][:])
         project(1)
         out_sb = keep.tile([P, P], F32)
         nc.vector.tensor_tensor(out=out_sb[:], in0=out_ps[:], in1=bo_sb[:], op=ALU.add)

@@ -23,8 +23,8 @@ BANK = 512
 PASSES = 2
 PACK = 4
 PAIR_COLS = 2 * D
-HALF = H // 2
-HALF_COLS = HALF * D
+PAIRS = H // 2
+SHARE_COLS = 64
 SCALE = D ** -0.5
 
 FLOPS = 2 * H * S * KEYS * D * 2 + 2 * S * HD * P
@@ -50,41 +50,43 @@ def tile_knnxlmultiheadsattention_pb_s_kernel(tc, q, qkv, kv_external, gate, Wo,
         ident_f32 = keep.tile([P, P], F32)
         make_identity(nc, ident_f32[:])
 
-        k0_sb = [keep.tile([P, 2, PAIR_COLS], BF16, name="k0_sb%d" % w) for w in range(T // 2)]
-        k1_sb = keep.tile([P, T, PAIR_COLS], BF16)
-        kb_sb = [keep.tile([P, PACK, HALF_COLS], BF16, name="kb_sb%d" % g) for g in range(PASSES)]
-        v_sb = [
-            [keep.tile([P, PACK, HALF_COLS], BF16, name="v_sb%d%d" % (f, g)) for g in range(PASSES)] for f in range(2)
-        ]
+        k_sb = [keep.tile([P, T, PAIR_COLS], BF16, name="k_sb%d" % c) for c in range(PAIRS)]
+        v_sb = [keep.tile([P, T, PAIR_COLS], BF16, name="v_sb%d" % c) for c in range(PAIRS)]
         q_sb = keep.tile([P, H, D], BF16)
         gate_sb = keep.tile([P, H], BF16)
         qkv_sb = keep.tile([P, H, D], BF16)
         wo_sb = keep.tile([P, HD], BF16)
         bo_sb = keep.tile([P, P], BF16)
-        half_cols = [slice(f * HALF_COLS, (f + 1) * HALF_COLS) for f in range(2)]
-        pass_ts = [slice(g * PACK, (g + 1) * PACK) for g in range(PASSES)]
 
-        for w in range(T // 2):
-            nc.sync.dma_start(out=k0_sb[w][:], in_=kv[:, 2 * w : 2 * w + 2, 0, 0:PAIR_COLS])
-            if w == 0:
-                nc.sync.dma_start(out=q_sb[:, 0:2, :], in_=q_rows[:, 0:2, :])
-        nc.sync.dma_start(out=k1_sb[:], in_=kv[:, :, 0, PAIR_COLS : 2 * PAIR_COLS])
+        def load_keys(c, lo, hi):
+            nc.sync.dma_start(out=k_sb[c][:, lo:hi, :], in_=kv[:, lo:hi, 0, c * PAIR_COLS : (c + 1) * PAIR_COLS])
+
+        def load_values(c, lo, hi):
+            nc.sync.dma_start(out=v_sb[c][:, lo:hi, :], in_=kv[:, lo:hi, 1, c * PAIR_COLS : (c + 1) * PAIR_COLS])
+
+        load_keys(0, 0, 2)
+        nc.sync.dma_start(out=q_sb[:, 0:2, :], in_=q_rows[:, 0:2, :])
+        load_keys(0, 2, 4)
+        load_keys(0, 4, 6)
+        load_keys(0, 6, 8)
+        load_keys(1, 0, T)
         nc.sync.dma_start(out=q_sb[:, 2:H, :], in_=q_rows[:, 2:H, :])
+        load_values(0, 0, PACK)
+        load_values(0, PACK, T)
         nc.sync.dma_start(out=gate_sb[:], in_=gate.rearrange("h a b -> (h a b)").partition_broadcast(P))
-        for g in range(PASSES):
-            nc.sync.dma_start(out=v_sb[0][g][:], in_=kv[:, pass_ts[g], 1, half_cols[0]])
-        for g in range(PASSES):
-            nc.sync.dma_start(out=kb_sb[g][:], in_=kv[:, pass_ts[g], 0, half_cols[1]])
+        load_keys(2, 0, T)
+        load_values(1, 0, T)
         nc.sync.dma_start(out=qkv_sb[:], in_=qkv.rearrange("b h i d -> i (b h) d"))
-        for g in range(PASSES):
-            nc.sync.dma_start(out=v_sb[1][g][:], in_=kv[:, pass_ts[g], 1, half_cols[1]])
+        load_keys(3, 0, T)
+        load_values(2, 0, T)
+        load_values(3, 0, T)
         nc.sync.dma_start(out=wo_sb[:], in_=Wo)
         nc.sync.dma_start(out=bo_sb[:], in_=bo.partition_broadcast(P))
 
         s_ps, nb, e_sb, rs, dn, eT_ps, eT_grp, e_codes, e_scales, cf, pv_ps, kT_ps = (
             {}, {}, {}, {}, {}, {}, {}, {}, {}, {}, {}, {}
         )
-        v_grp, v_codes, v_scales = {}, {}, {}
+        v_grp, v_codes, v_scales, mx_both = {}, {}, {}, {}
         qT = keep.tile([P, H, S], BF16)
         kT = keep.tile([P, H, KEYS], BF16)
         den = keep.tile([P, 2 * H], F32)
@@ -102,7 +104,7 @@ def tile_knnxlmultiheadsattention_pb_s_kernel(tc, q, qkv, kv_external, gate, Wo,
             k_ps = psum.tile([P, 2, 2, P], BF16, tag="turned", bufs=3)
             for h in range(2):
                 for t in range(2):
-                    nc.tensor.transpose(k_ps[:, h, t, :], k0_sb[w][:, t, h * D : (h + 1) * D], ident_bf[:])
+                    nc.tensor.transpose(k_ps[:, h, t, :], k_sb[0][:, 2 * w + t, h * D : (h + 1) * D], ident_bf[:])
             copy(
                 out=kT[:, 0:2, 2 * w * P : (2 * w + 2) * P],
                 in_=k_ps[:].rearrange("p h t r -> p h (t r)"),
@@ -111,14 +113,11 @@ def tile_knnxlmultiheadsattention_pb_s_kernel(tc, q, qkv, kv_external, gate, Wo,
         def turn_keys(h):
             kT_ps[h] = psum.tile([P, T, P], BF16, name="kT_ps", tag="turned", bufs=3)
             for t in range(T):
-                if h < HALF:
-                    rows = k1_sb[:, t, (h - 2) * D : (h - 1) * D]
-                else:
-                    rows = kb_sb[t // PACK][:, t % PACK, (h - HALF) * D : (h - HALF + 1) * D]
+                rows = k_sb[h // 2][:, t, (h % 2) * D : (h % 2 + 1) * D]
                 nc.tensor.transpose(kT_ps[h][:, t, :], rows, ident_bf[:])
 
-        def keep_keys(h):
-            nc.scalar.copy(out=kT[:, h, :], in_=kT_ps[h][:].rearrange("p t r -> p (t r)"))
+        def keep_keys(copy, h):
+            copy(out=kT[:, h, :], in_=kT_ps[h][:].rearrange("p t r -> p (t r)"))
 
         def turn_words(turned, rows, first, count):
             words = rows.bitcast(F32)
@@ -144,9 +143,13 @@ def tile_knnxlmultiheadsattention_pb_s_kernel(tc, q, qkv, kv_external, gate, Wo,
             mx = work.tile([P, PASSES], F32, tag="mx")
             for g in range(PASSES):
                 nc.vector.reduce_max(out=mx[:, g : g + 1], in_=s_ps[h][g][:], axis=AX.X)
+            mx_both[h] = mx
+
+        def negate_max(h):
             nb[h] = work.tile([P, 1], F32, name="nb", tag="nb")
-            nc.gpsimd.tensor_scalar(
-                out=nb[h][:], in0=mx[:, 0:1], scalar1=mx[:, 1:2], scalar2=-SCALE, op0=ALU.max, op1=ALU.mult
+            nc.vector.tensor_scalar(
+                out=nb[h][:], in0=mx_both[h][:, 0:1], scalar1=mx_both[h][:, 1:2], scalar2=-SCALE,
+                op0=ALU.max, op1=ALU.mult,
             )
 
         def exponentials(h, g):
@@ -175,18 +178,25 @@ def tile_knnxlmultiheadsattention_pb_s_kernel(tc, q, qkv, kv_external, gate, Wo,
                 op0=ALU.mult, op1=ALU.add,
             )
 
-        def turn_e(h):
-            eT_ps[h] = psum.tile([P, 2 * PASSES, P], F32, name="eT_ps", tag="turned", bufs=3)
-            turn_words(eT_ps[h], e_sb[h][:], 0, 2 * PASSES)
+        def turn_e(h, g, count, tag, bufs):
+            eT_ps[h, g] = psum.tile([P, 2 * count, P], F32, name="eT_ps", tag=tag, bufs=bufs)
+            turn_words(eT_ps[h, g], e_sb[h][:], 2 * g, 2 * count)
 
-        def keep_e(h):
-            eT_grp[h] = work.tile([P, KEYS], BF16, name="eT_grp", tag="eT_grp", align_bytes=64)
-            regroup_words(nc.scalar.copy, eT_grp[h][:], eT_ps[h][:])
+        def keep_e(copy, h, g, count):
+            if g == 0:
+                eT_grp[h] = work.tile([P, KEYS], BF16, name="eT_grp", tag="eT_grp", align_bytes=64)
+            regroup_words(copy, eT_grp[h][:, g * BANK : (g + count) * BANK], eT_ps[h, g][:])
 
-        def quantise_e(h):
-            e_codes[h] = work.tile([P, PASSES * P], U32, name="e_codes", tag="e_codes", align_bytes=64)
-            e_scales[h] = work.tile([P, PASSES * P], U8, name="e_scales", tag="e_scales", align_bytes=64)
-            nc.vector.quantize_mx(out=e_codes[h][:].bitcast(FP8X4), scales=e_scales[h][:], in_=eT_grp[h][:])
+        def quantise_e(h, g, count):
+            if g == 0:
+                e_codes[h] = work.tile([P, PASSES * P], U32, name="e_codes", tag="e_codes", align_bytes=64)
+                e_scales[h] = work.tile([P, PASSES * P], U8, name="e_scales", tag="e_scales", align_bytes=64)
+            words = slice(g * P, (g + count) * P)
+            nc.vector.quantize_mx(
+                out=e_codes[h][:, words].bitcast(FP8X4),
+                scales=e_scales[h][:, words],
+                in_=eT_grp[h][:, g * BANK : (g + count) * BANK],
+            )
 
         def invert_sum(h):
             cf[h] = work.tile([P, 1], F32, name="cf", tag="cf")
@@ -200,8 +210,8 @@ def tile_knnxlmultiheadsattention_pb_s_kernel(tc, q, qkv, kv_external, gate, Wo,
                     out=pv_ps[h][:],
                     lhsT=e_codes[h][:, g * P : (g + 1) * P].bitcast(FP8X4),
                     lhsT_scale=e_scales[h][:, g * P : (g + 1) * P],
-                    rhs=v_codes[h // 2, g][:, cols].bitcast(FP8X4),
-                    rhs_scale=v_scales[h // 2, g][:, cols],
+                    rhs=v_codes[h // 2][:, g, cols].bitcast(FP8X4),
+                    rhs_scale=v_scales[h // 2][:, g, cols],
                     start=(g == 0),
                     stop=(g == PASSES - 1),
                 )
@@ -212,26 +222,39 @@ def tile_knnxlmultiheadsattention_pb_s_kernel(tc, q, qkv, kv_external, gate, Wo,
                 op0=ALU.mult, op1=ALU.add,
             )
 
+        for c in range(PAIRS):
+            v_grp[c] = keep.tile([P, PASSES, PAIR_COLS, PACK], BF16, name="v_grp%d" % c, align_bytes=64)
+
         def regroup_values(copy, c, g):
-            v_grp[c, g] = keep.tile([P, PAIR_COLS, PACK], BF16, name="v_grp%d%d" % (c, g), align_bytes=64)
-            cols = slice((c % 2) * PAIR_COLS, (c % 2 + 1) * PAIR_COLS)
             copy(
-                out=v_grp[c, g][:].rearrange("p (c i) t -> p c t i", i=4),
-                in_=v_sb[c // 2][g][:, :, cols].rearrange("p t (c i) -> p c t i", i=4),
+                out=v_grp[c][:, g].rearrange("p (c i) t -> p c t i", i=4),
+                in_=v_sb[c][:, g * PACK : (g + 1) * PACK, :].rearrange("p t (c i) -> p c t i", i=4),
             )
 
-        def quantise_values(c, g):
-            v_codes[c, g] = keep.tile([P, PAIR_COLS], U32, name="v_codes%d%d" % (c, g), align_bytes=64)
-            v_scales[c, g] = keep.tile([P, PAIR_COLS], U8, name="v_scales%d%d" % (c, g), align_bytes=64)
+        def regroup_values_gpsimd(c, g):
+            for lo in range(0, PAIR_COLS, SHARE_COLS):
+                nc.gpsimd.tensor_scalar(
+                    out=v_grp[c][:, g, lo : lo + SHARE_COLS, :].rearrange("p (c i) t -> p c t i", i=4),
+                    in0=v_sb[c][:, g * PACK : (g + 1) * PACK, lo : lo + SHARE_COLS].rearrange("p t (c i) -> p c t i", i=4),
+                    scalar1=1.0,
+                    scalar2=0.0,
+                    op0=ALU.mult,
+                    op1=ALU.add,
+                )
+
+        def quantise_values(c):
+            v_codes[c] = keep.tile([P, PASSES, PAIR_COLS], U32, name="v_codes%d" % c, align_bytes=64)
+            v_scales[c] = keep.tile([P, PASSES, PAIR_COLS], U8, name="v_scales%d" % c, align_bytes=64)
             nc.vector.quantize_mx(
-                out=v_codes[c, g][:].bitcast(FP8X4),
-                scales=v_scales[c, g][:],
-                in_=v_grp[c, g][:].rearrange("p c t -> p (c t)"),
+                out=v_codes[c][:].rearrange("p g c -> p (g c)").bitcast(FP8X4),
+                scales=v_scales[c][:].rearrange("p g c -> p (g c)"),
+                in_=v_grp[c][:].rearrange("p g c t -> p (g c t)"),
             )
 
         def is_head(h):
             return 0 <= h < H
 
+        last = H - 1
         turn_first_keys(nc.vector.tensor_copy, 0)
         turn_q(nc.scalar.copy, 0, 2)
         turn_first_keys(nc.scalar.copy, 1)
@@ -239,70 +262,82 @@ def tile_knnxlmultiheadsattention_pb_s_kernel(tc, q, qkv, kv_external, gate, Wo,
         turn_first_keys(nc.scalar.copy, 3)
         scores(0)
         row_max(0)
+        negate_max(0)
         scores(1)
         turn_keys(2)
-        keep_keys(2)
-        turn_q(nc.scalar.copy, 2, H)
+        row_max(1)
+        turn_q(nc.vector.tensor_copy, 2, H)
+        negate_max(1)
+        keep_keys(nc.vector.tensor_copy, 2)
         turn_keys(3)
+        regroup_values(nc.vector.tensor_copy, 0, 0)
 
         for r in range(H):
-            if is_head(r + 1):
-                row_max(r + 1)
-            if is_head(r - 2):
-                fuse(r - 2)
             exponentials(r, 0)
+            if r == last:
+                turn_e(r, 0, 1, "s", 4)
             exponentials(r, 1)
             if is_head(r + 2):
                 scores(r + 2)
-            turn_e(r)
+            if r < last:
+                turn_e(r, 0, PASSES, "turned", 3)
+            else:
+                turn_e(r, 1, 1, "s", 4)
             if is_head(r - 1):
-                keep_e(r - 1)
+                keep_e(nc.scalar.copy, r - 1, 0, PASSES)
             if is_head(r + 3):
-                keep_keys(r + 3)
+                keep_keys(nc.scalar.copy, r + 3)
+            if is_head(r + 4):
+                turn_keys(r + 4)
+            if r == 0:
+                nc.scalar.activation(out=den[:, 0:H], in_=gate_sb[:], func=ACT.Exp, scale=-1.0)
+                nc.scalar.activation(out=den[:, H : 2 * H], in_=gate_sb[:], func=ACT.Exp, scale=1.0)
             if r == 5:
                 w_grp = keep.tile([P, HD], BF16, align_bytes=64)
                 regroup_words(nc.scalar.copy, w_grp[:], w_ps[:])
                 m_grp = [keep.tile([P, BANK], BF16, name="m_grp%d" % g, align_bytes=64) for g in range(PASSES)]
                 m_codes = [keep.tile([P, P], U32, name="m_codes%d" % g, align_bytes=64) for g in range(PASSES)]
                 m_scales = [keep.tile([P, P], U8, name="m_scales%d" % g, align_bytes=64) for g in range(PASSES)]
-            if r == 7:
+            if r == 6:
                 regroup_words(nc.scalar.copy, m_grp[0][:], m0_ps[:])
-            c = (r + 1) // 2
-            if r == 0:
-                nc.scalar.activation(out=den[:, 0:H], in_=gate_sb[:], func=ACT.Exp, scale=-1.0)
-                nc.scalar.activation(out=den[:, H : 2 * H], in_=gate_sb[:], func=ACT.Exp, scale=1.0)
-                regroup_values(nc.vector.tensor_copy, 0, 0)
-                regroup_values(nc.vector.tensor_copy, 0, 1)
+            if 0 < r and is_head(r + 1):
+                row_max(r + 1)
+            if r == 1:
                 nc.vector.tensor_scalar_add(out=den[:], in0=den[:], scalar1=1.0)
-                quantise_values(0, 0)
+            if is_head(r - 2):
+                fuse(r - 2)
+            if 0 < r and is_head(r + 1):
+                negate_max(r + 1)
+            if r == 1:
                 nc.vector.reciprocal(out=g_sb[:], in_=den[:, 0:H])
-                quantise_values(0, 1)
-            elif r % 2 == 1:
-                if c < H // 2:
-                    regroup_values(nc.vector.tensor_copy, c, 0)
-            else:
-                regroup_values(nc.vector.tensor_copy, c, 1)
-                quantise_values(c, 0)
-            if is_head(r - 1):
-                scale_sum(r - 1)
-                gate_local(r - 1)
-                invert_sum(r - 1)
-                quantise_e(r - 1)
-                weighted_values(r - 1)
-            if r > 0 and r % 2 == 0:
-                quantise_values(c, 1)
             if r == 6:
                 w_codes = keep.tile([P, PASSES * P], U32, align_bytes=64)
                 w_scales = keep.tile([P, PASSES * P], U8, align_bytes=64)
                 nc.vector.quantize_mx(out=w_codes[:].bitcast(FP8X4), scales=w_scales[:], in_=w_grp[:])
-            if is_head(r + 4):
-                turn_keys(r + 4)
             if r == 4:
                 w_ps = psum.tile([P, 2 * PASSES, P], F32, tag="turned", bufs=3)
                 turn_words(w_ps, wo_sb[:], 0, 2 * PASSES)
-            if r == 6:
+            if r == 5:
                 m0_ps = psum.tile([P, 2, P], F32, tag="turned", bufs=3)
                 turn_words(m0_ps, merged[:], 0, 2)
+            c = r // 2
+            if r > 0:
+                if c < PAIRS - 1:
+                    regroup_values(nc.vector.tensor_copy, c, r % 2)
+                if r == last - 1:
+                    quantise_values(PAIRS - 1)
+                quantise_e(r - 1, 0, PASSES)
+                if r % 2 == 1 and r < last:
+                    quantise_values(c)
+                scale_sum(r - 1)
+                gate_local(r - 1)
+                invert_sum(r - 1)
+                if r in (4, 5):
+                    regroup_values_gpsimd(PAIRS - 1, r - 4)
+                weighted_values(r - 1)
+
+        def quantise_merged(g):
+            nc.vector.quantize_mx(out=m_codes[g][:].bitcast(FP8X4), scales=m_scales[g][:], in_=m_grp[g][:])
 
         def project(g):
             nc.tensor.matmul_mx(
@@ -315,14 +350,15 @@ def tile_knnxlmultiheadsattention_pb_s_kernel(tc, q, qkv, kv_external, gate, Wo,
                 stop=(g == PASSES - 1),
             )
 
-        last = H - 1
-        keep_e(last)
-        nc.vector.quantize_mx(out=m_codes[0][:].bitcast(FP8X4), scales=m_scales[0][:], in_=m_grp[0][:])
+        keep_e(nc.vector.tensor_copy, last, 0, 1)
+        keep_e(nc.scalar.copy, last, 1, 1)
         fuse(last - 1)
+        quantise_e(last, 0, 1)
         scale_sum(last)
         gate_local(last)
         invert_sum(last)
-        quantise_e(last)
+        quantise_e(last, 1, 1)
+        quantise_merged(0)
         weighted_values(last)
         out_ps = psum.tile([P, P], F32, tag="s", bufs=4)
         project(0)
@@ -330,7 +366,7 @@ def tile_knnxlmultiheadsattention_pb_s_kernel(tc, q, qkv, kv_external, gate, Wo,
         m1_ps = psum.tile([P, 2, P], F32, tag="turned", bufs=3)
         turn_words(m1_ps, merged[:], 2, 2)
         regroup_words(nc.vector.tensor_copy, m_grp[1][:], m1_ps[:])
-        nc.vector.quantize_mx(out=m_codes[1][:].bitcast(FP8X4), scales=m_scales[1][:], in_=m_grp[1][:])
+        quantise_merged(1)
         project(1)
         out_sb = keep.tile([P, P], F32)
         nc.vector.tensor_tensor(out=out_sb[:], in0=out_ps[:], in1=bo_sb[:], op=ALU.add)

@@ -69,8 +69,9 @@ def tile_knnxlmultiheadsattention_pb_s_kernel(tc, q, qkv, kv_external, gate, Wo,
         load_keys(0, 2, 4)
         load_keys(0, 4, 6)
         load_keys(0, 6, 8)
+        nc.sync.dma_start(out=q_sb[:, 2:4, :], in_=q_rows[:, 2:4, :])
         load_keys(1, 0, T)
-        nc.sync.dma_start(out=q_sb[:, 2:H, :], in_=q_rows[:, 2:H, :])
+        nc.sync.dma_start(out=q_sb[:, 4:H, :], in_=q_rows[:, 4:H, :])
         load_values(0, 0, PACK)
         load_values(0, PACK, T)
         nc.sync.dma_start(out=gate_sb[:], in_=gate.rearrange("h a b -> (h a b)").partition_broadcast(P))
@@ -203,7 +204,10 @@ def tile_knnxlmultiheadsattention_pb_s_kernel(tc, q, qkv, kv_external, gate, Wo,
             nc.vector.reciprocal(out=cf[h][:], in_=dn[h][:])
 
         def weighted_values(h):
-            pv_ps[h] = psum.tile([P, D], F32, name="pv_ps", tag="pv", bufs=1)
+            if h < H - 1:
+                pv_ps[h] = psum.tile([P, D], F32, name="pv_ps", tag="pv", bufs=1)
+            else:
+                pv_ps[h] = psum.tile([P, D], F32, name="pv_ps", tag="s", bufs=4)
             cols = slice((h % 2) * D, (h % 2 + 1) * D)
             for g in range(PASSES):
                 nc.tensor.matmul_mx(
@@ -263,14 +267,16 @@ def tile_knnxlmultiheadsattention_pb_s_kernel(tc, q, qkv, kv_external, gate, Wo,
         scores(0)
         row_max(0)
         negate_max(0)
-        scores(1)
+        turn_q(nc.scalar.copy, 2, 4)
         turn_keys(2)
+        keep_keys(nc.scalar.copy, 2)
+        scores(1)
         row_max(1)
-        turn_q(nc.vector.tensor_copy, 2, H)
         negate_max(1)
-        keep_keys(nc.vector.tensor_copy, 2)
         turn_keys(3)
+        turn_q(nc.vector.tensor_copy, 4, H)
         regroup_values(nc.vector.tensor_copy, 0, 0)
+        regroup_values(nc.vector.tensor_copy, 0, 1)
 
         for r in range(H):
             exponentials(r, 0)
@@ -283,12 +289,12 @@ def tile_knnxlmultiheadsattention_pb_s_kernel(tc, q, qkv, kv_external, gate, Wo,
                 turn_e(r, 0, PASSES, "turned", 3)
             else:
                 turn_e(r, 1, 1, "s", 4)
+            if is_head(r - 2):
+                weighted_values(r - 2)
             if is_head(r - 1):
                 keep_e(nc.scalar.copy, r - 1, 0, PASSES)
             if is_head(r + 3):
                 keep_keys(nc.scalar.copy, r + 3)
-            if is_head(r + 4):
-                turn_keys(r + 4)
             if r == 0:
                 nc.scalar.activation(out=den[:, 0:H], in_=gate_sb[:], func=ACT.Exp, scale=-1.0)
                 nc.scalar.activation(out=den[:, H : 2 * H], in_=gate_sb[:], func=ACT.Exp, scale=1.0)
@@ -298,43 +304,45 @@ def tile_knnxlmultiheadsattention_pb_s_kernel(tc, q, qkv, kv_external, gate, Wo,
                 m_grp = [keep.tile([P, BANK], BF16, name="m_grp%d" % g, align_bytes=64) for g in range(PASSES)]
                 m_codes = [keep.tile([P, P], U32, name="m_codes%d" % g, align_bytes=64) for g in range(PASSES)]
                 m_scales = [keep.tile([P, P], U8, name="m_scales%d" % g, align_bytes=64) for g in range(PASSES)]
-            if r == 6:
+            if r == 7:
                 regroup_words(nc.scalar.copy, m_grp[0][:], m0_ps[:])
-            if 0 < r and is_head(r + 1):
-                row_max(r + 1)
-            if r == 1:
+            if is_head(r + 2):
+                row_max(r + 2)
+            if r == 0:
                 nc.vector.tensor_scalar_add(out=den[:], in0=den[:], scalar1=1.0)
-            if is_head(r - 2):
-                fuse(r - 2)
-            if 0 < r and is_head(r + 1):
-                negate_max(r + 1)
-            if r == 1:
+            if r > 0:
+                scale_sum(r - 1)
+                invert_sum(r - 1)
+            if is_head(r + 2):
+                negate_max(r + 2)
+            if r == 0:
                 nc.vector.reciprocal(out=g_sb[:], in_=den[:, 0:H])
-            if r == 6:
-                w_codes = keep.tile([P, PASSES * P], U32, align_bytes=64)
-                w_scales = keep.tile([P, PASSES * P], U8, align_bytes=64)
-                nc.vector.quantize_mx(out=w_codes[:].bitcast(FP8X4), scales=w_scales[:], in_=w_grp[:])
+            if is_head(r + 4):
+                turn_keys(r + 4)
             if r == 4:
                 w_ps = psum.tile([P, 2 * PASSES, P], F32, tag="turned", bufs=3)
                 turn_words(w_ps, wo_sb[:], 0, 2 * PASSES)
-            if r == 5:
-                m0_ps = psum.tile([P, 2, P], F32, tag="turned", bufs=3)
-                turn_words(m0_ps, merged[:], 0, 2)
             c = r // 2
+            if 0 < r < 5:
+                regroup_values(nc.vector.tensor_copy, (r + 1) // 2, (r + 1) % 2)
             if r > 0:
-                if c < PAIRS - 1:
-                    regroup_values(nc.vector.tensor_copy, c, r % 2)
-                if r == last - 1:
-                    quantise_values(PAIRS - 1)
                 quantise_e(r - 1, 0, PASSES)
                 if r % 2 == 1 and r < last:
                     quantise_values(c)
-                scale_sum(r - 1)
+                if r == last - 1:
+                    quantise_values(PAIRS - 1)
+                if r == last:
+                    w_codes = keep.tile([P, PASSES * P], U32, align_bytes=64)
+                    w_scales = keep.tile([P, PASSES * P], U8, align_bytes=64)
+                    nc.vector.quantize_mx(out=w_codes[:].bitcast(FP8X4), scales=w_scales[:], in_=w_grp[:])
+                if is_head(r - 2):
+                    fuse(r - 2)
+                if r == 6:
+                    m0_ps = psum.tile([P, 2, P], F32, tag="turned", bufs=3)
+                    turn_words(m0_ps, merged[:], 0, 2)
                 gate_local(r - 1)
-                invert_sum(r - 1)
                 if r in (4, 5):
                     regroup_values_gpsimd(PAIRS - 1, r - 4)
-                weighted_values(r - 1)
 
         def quantise_merged(g):
             nc.vector.quantize_mx(out=m_codes[g][:].bitcast(FP8X4), scales=m_scales[g][:], in_=m_grp[g][:])
@@ -350,15 +358,16 @@ def tile_knnxlmultiheadsattention_pb_s_kernel(tc, q, qkv, kv_external, gate, Wo,
                 stop=(g == PASSES - 1),
             )
 
+        weighted_values(last - 1)
         keep_e(nc.vector.tensor_copy, last, 0, 1)
         keep_e(nc.scalar.copy, last, 1, 1)
-        fuse(last - 1)
-        quantise_e(last, 0, 1)
         scale_sum(last)
         gate_local(last)
+        quantise_merged(0)
+        quantise_e(last, 0, 1)
         invert_sum(last)
         quantise_e(last, 1, 1)
-        quantise_merged(0)
+        fuse(last - 1)
         weighted_values(last)
         out_ps = psum.tile([P, P], F32, tag="s", bufs=4)
         project(0)

@@ -167,9 +167,10 @@ def tile_knnxlmultiheadsattention_pb_s_kernel(tc, q, qkv, kv_external, gate, Wo,
             )
 
         def scale_sum(h):
-            dn[h] = work.tile([P, 1], F32, name="dn", tag="dn")
+            if h % 2 == 0:
+                dn[h // 2] = work.tile([P, 2], F32, name="dn", tag="dn")
             nc.gpsimd.tensor_scalar(
-                out=dn[h][:], in0=rs[h][:, 0:1], scalar1=rs[h][:, 1:2], scalar2=den[:, H + h : H + h + 1],
+                out=dn[h // 2][:, h % 2 : h % 2 + 1], in0=rs[h][:, 0:1], scalar1=rs[h][:, 1:2], scalar2=den[:, H + h : H + h + 1],
                 op0=ALU.add, op1=ALU.mult,
             )
 
@@ -199,9 +200,9 @@ def tile_knnxlmultiheadsattention_pb_s_kernel(tc, q, qkv, kv_external, gate, Wo,
                 in_=eT_grp[h][:, g * BANK : (g + count) * BANK],
             )
 
-        def invert_sum(h):
-            cf[h] = work.tile([P, 1], F32, name="cf", tag="cf")
-            nc.vector.reciprocal(out=cf[h][:], in_=dn[h][:])
+        def invert_sums(c):
+            cf[c] = work.tile([P, 2], F32, name="cf", tag="cf")
+            nc.vector.reciprocal(out=cf[c][:], in_=dn[c][:])
 
         def weighted_values(h):
             if h < H - 1:
@@ -222,29 +223,29 @@ def tile_knnxlmultiheadsattention_pb_s_kernel(tc, q, qkv, kv_external, gate, Wo,
 
         def fuse(h):
             nc.vector.scalar_tensor_tensor(
-                out=merged[:, h * D : (h + 1) * D], in0=pv_ps[h][:], scalar=cf[h][:, 0:1], in1=qg[:, h, :],
+                out=merged[:, h * D : (h + 1) * D], in0=pv_ps[h][:], scalar=cf[h // 2][:, h % 2 : h % 2 + 1], in1=qg[:, h, :],
                 op0=ALU.mult, op1=ALU.add,
             )
 
         for c in range(PAIRS):
             v_grp[c] = keep.tile([P, PASSES, PAIR_COLS, PACK], BF16, name="v_grp%d" % c, align_bytes=64)
 
-        def regroup_values(copy, c, g):
+        def regroup_values(copy, c, g, lo, hi):
             copy(
-                out=v_grp[c][:, g].rearrange("p (c i) t -> p c t i", i=4),
-                in_=v_sb[c][:, g * PACK : (g + 1) * PACK, :].rearrange("p t (c i) -> p c t i", i=4),
+                out=v_grp[c][:, g, lo:hi, :].rearrange("p (c i) t -> p c t i", i=4),
+                in_=v_sb[c][:, g * PACK : (g + 1) * PACK, lo:hi].rearrange("p t (c i) -> p c t i", i=4),
             )
 
-        def regroup_values_gpsimd(c, g):
-            for lo in range(0, PAIR_COLS, SHARE_COLS):
-                nc.gpsimd.tensor_scalar(
-                    out=v_grp[c][:, g, lo : lo + SHARE_COLS, :].rearrange("p (c i) t -> p c t i", i=4),
-                    in0=v_sb[c][:, g * PACK : (g + 1) * PACK, lo : lo + SHARE_COLS].rearrange("p t (c i) -> p c t i", i=4),
-                    scalar1=1.0,
-                    scalar2=0.0,
-                    op0=ALU.mult,
-                    op1=ALU.add,
-                )
+        def regroup_share(c, g, share):
+            cols = slice(share * SHARE_COLS, (share + 1) * SHARE_COLS)
+            nc.gpsimd.tensor_scalar(
+                out=v_grp[c][:, g, cols, :].rearrange("p (c i) t -> p c t i", i=4),
+                in0=v_sb[c][:, g * PACK : (g + 1) * PACK, cols].rearrange("p t (c i) -> p c t i", i=4),
+                scalar1=1.0,
+                scalar2=0.0,
+                op0=ALU.mult,
+                op1=ALU.add,
+            )
 
         def quantise_values(c):
             v_codes[c] = keep.tile([P, PASSES, PAIR_COLS], U32, name="v_codes%d" % c, align_bytes=64)
@@ -275,9 +276,12 @@ def tile_knnxlmultiheadsattention_pb_s_kernel(tc, q, qkv, kv_external, gate, Wo,
         negate_max(1)
         turn_keys(3)
         turn_q(nc.vector.tensor_copy, 4, H)
-        regroup_values(nc.vector.tensor_copy, 0, 0)
-        regroup_values(nc.vector.tensor_copy, 0, 1)
+        regroup_values(nc.vector.tensor_copy, 0, 0, 0, PAIR_COLS)
+        regroup_values(nc.vector.tensor_copy, 0, 1, 0, PAIR_COLS)
 
+        VREGS = {1:[[1,0,0,256]],2:[[1,1,128,256]],3:[[2,0,0,256]],6:[[3,1,0,256]]}
+        SHARES = {1:[[1,1,0],[1,1,1]],3:[[2,1,0],[2,1,1]],4:[[2,1,2],[2,1,3]],5:[[3,0,0],[3,0,1],[3,0,2],[3,0,3]]}
+        K_ON_VECTOR = (4, 6,)
         for r in range(H):
             exponentials(r, 0)
             if r == last:
@@ -293,7 +297,7 @@ def tile_knnxlmultiheadsattention_pb_s_kernel(tc, q, qkv, kv_external, gate, Wo,
                 weighted_values(r - 2)
             if is_head(r - 1):
                 keep_e(nc.scalar.copy, r - 1, 0, PASSES)
-            if is_head(r + 3):
+            if is_head(r + 3) and r + 3 not in K_ON_VECTOR:
                 keep_keys(nc.scalar.copy, r + 3)
             if r == 0:
                 nc.scalar.activation(out=den[:, 0:H], in_=gate_sb[:], func=ACT.Exp, scale=-1.0)
@@ -306,13 +310,16 @@ def tile_knnxlmultiheadsattention_pb_s_kernel(tc, q, qkv, kv_external, gate, Wo,
                 m_scales = [keep.tile([P, P], U8, name="m_scales%d" % g, align_bytes=64) for g in range(PASSES)]
             if r == 7:
                 regroup_words(nc.scalar.copy, m_grp[0][:], m0_ps[:])
+            if r + 3 in K_ON_VECTOR:
+                keep_keys(nc.vector.tensor_copy, r + 3)
             if is_head(r + 2):
                 row_max(r + 2)
             if r == 0:
                 nc.vector.tensor_scalar_add(out=den[:], in0=den[:], scalar1=1.0)
             if r > 0:
                 scale_sum(r - 1)
-                invert_sum(r - 1)
+                if r % 2 == 0:
+                    invert_sums(r // 2 - 1)
             if is_head(r + 2):
                 negate_max(r + 2)
             if r == 0:
@@ -323,14 +330,14 @@ def tile_knnxlmultiheadsattention_pb_s_kernel(tc, q, qkv, kv_external, gate, Wo,
                 w_ps = psum.tile([P, 2 * PASSES, P], F32, tag="turned", bufs=3)
                 turn_words(w_ps, wo_sb[:], 0, 2 * PASSES)
             c = r // 2
-            if 0 < r < 5:
-                regroup_values(nc.vector.tensor_copy, (r + 1) // 2, (r + 1) % 2)
+            for vc, vg, lo, hi in VREGS.get(r, ()):
+                regroup_values(nc.vector.tensor_copy, vc, vg, lo, hi)
             if r > 0:
+                if r == 7:
+                    quantise_values(PAIRS - 1)
                 quantise_e(r - 1, 0, PASSES)
                 if r % 2 == 1 and r < last:
                     quantise_values(c)
-                if r == last - 1:
-                    quantise_values(PAIRS - 1)
                 if r == last:
                     w_codes = keep.tile([P, PASSES * P], U32, align_bytes=64)
                     w_scales = keep.tile([P, PASSES * P], U8, align_bytes=64)
@@ -341,8 +348,8 @@ def tile_knnxlmultiheadsattention_pb_s_kernel(tc, q, qkv, kv_external, gate, Wo,
                     m0_ps = psum.tile([P, 2, P], F32, tag="turned", bufs=3)
                     turn_words(m0_ps, merged[:], 0, 2)
                 gate_local(r - 1)
-                if r in (4, 5):
-                    regroup_values_gpsimd(PAIRS - 1, r - 4)
+                for gc, gg, gs in SHARES.get(r, ()):
+                    regroup_share(gc, gg, gs)
 
         def quantise_merged(g):
             nc.vector.quantize_mx(out=m_codes[g][:].bitcast(FP8X4), scales=m_scales[g][:], in_=m_grp[g][:])
@@ -365,7 +372,7 @@ def tile_knnxlmultiheadsattention_pb_s_kernel(tc, q, qkv, kv_external, gate, Wo,
         gate_local(last)
         quantise_merged(0)
         quantise_e(last, 0, 1)
-        invert_sum(last)
+        invert_sums(last // 2)
         quantise_e(last, 1, 1)
         fuse(last - 1)
         weighted_values(last)

@@ -99,7 +99,7 @@ def tile_knnxlmultiheadsattention_pb_s_kernel(tc, q, qkv, kv_external, gate, Wo,
             q_ps = psum.tile([P, H, P], BF16, tag="turned", bufs=3)
             for h in range(lo, hi):
                 nc.tensor.transpose(q_ps[:, h, :], q_sb[:, h, :], ident_bf[:])
-            copy(out=qT[:, lo:hi, :], in_=q_ps[:, lo:hi, :])
+            copy(out=qT[:, lo:hi, :].bitcast(F32), in_=q_ps[:, lo:hi, :].bitcast(F32))
 
         def turn_first_keys(copy, w):
             k_ps = psum.tile([P, 2, 2, P], BF16, tag="turned", bufs=3)
@@ -107,8 +107,8 @@ def tile_knnxlmultiheadsattention_pb_s_kernel(tc, q, qkv, kv_external, gate, Wo,
                 for t in range(2):
                     nc.tensor.transpose(k_ps[:, h, t, :], k_sb[0][:, 2 * w + t, h * D : (h + 1) * D], ident_bf[:])
             copy(
-                out=kT[:, 0:2, 2 * w * P : (2 * w + 2) * P],
-                in_=k_ps[:].rearrange("p h t r -> p h (t r)"),
+                out=kT[:, 0:2, 2 * w * P : (2 * w + 2) * P].bitcast(F32),
+                in_=k_ps[:].rearrange("p h t r -> p h (t r)").bitcast(F32),
             )
 
         def turn_keys(h):
@@ -118,7 +118,7 @@ def tile_knnxlmultiheadsattention_pb_s_kernel(tc, q, qkv, kv_external, gate, Wo,
                 nc.tensor.transpose(kT_ps[h][:, t, :], rows, ident_bf[:])
 
         def keep_keys(copy, h):
-            copy(out=kT[:, h, :], in_=kT_ps[h][:].rearrange("p t r -> p (t r)"))
+            copy(out=kT[:, h, :].bitcast(F32), in_=kT_ps[h][:].rearrange("p t r -> p (t r)").bitcast(F32))
 
         def turn_words(turned, rows, first, count):
             words = rows.bitcast(F32)
@@ -264,7 +264,7 @@ def tile_knnxlmultiheadsattention_pb_s_kernel(tc, q, qkv, kv_external, gate, Wo,
         turn_q(nc.scalar.copy, 0, 2)
         turn_first_keys(nc.scalar.copy, 1)
         turn_first_keys(nc.vector.tensor_copy, 2)
-        turn_first_keys(nc.scalar.copy, 3)
+        turn_first_keys(nc.vector.tensor_copy, 3)
         scores(0)
         row_max(0)
         negate_max(0)
@@ -281,7 +281,6 @@ def tile_knnxlmultiheadsattention_pb_s_kernel(tc, q, qkv, kv_external, gate, Wo,
 
         VREGS = {1:[[1,0,0,256]],2:[[1,1,128,256]],3:[[2,0,0,256]],6:[[3,1,0,256]]}
         SHARES = {1:[[1,1,0],[1,1,1]],3:[[2,1,0],[2,1,1]],4:[[2,1,2],[2,1,3]],5:[[3,0,0],[3,0,1],[3,0,2],[3,0,3]]}
-        K_ON_VECTOR = (4, 6,)
         for r in range(H):
             exponentials(r, 0)
             if r == last:
@@ -297,7 +296,7 @@ def tile_knnxlmultiheadsattention_pb_s_kernel(tc, q, qkv, kv_external, gate, Wo,
                 weighted_values(r - 2)
             if is_head(r - 1):
                 keep_e(nc.scalar.copy, r - 1, 0, PASSES)
-            if is_head(r + 3) and r + 3 not in K_ON_VECTOR:
+            if is_head(r + 3):
                 keep_keys(nc.scalar.copy, r + 3)
             if r == 0:
                 nc.scalar.activation(out=den[:, 0:H], in_=gate_sb[:], func=ACT.Exp, scale=-1.0)
@@ -308,10 +307,6 @@ def tile_knnxlmultiheadsattention_pb_s_kernel(tc, q, qkv, kv_external, gate, Wo,
                 m_grp = [keep.tile([P, BANK], BF16, name="m_grp%d" % g, align_bytes=64) for g in range(PASSES)]
                 m_codes = [keep.tile([P, P], U32, name="m_codes%d" % g, align_bytes=64) for g in range(PASSES)]
                 m_scales = [keep.tile([P, P], U8, name="m_scales%d" % g, align_bytes=64) for g in range(PASSES)]
-            if r == 7:
-                regroup_words(nc.scalar.copy, m_grp[0][:], m0_ps[:])
-            if r + 3 in K_ON_VECTOR:
-                keep_keys(nc.vector.tensor_copy, r + 3)
             if is_head(r + 2):
                 row_max(r + 2)
             if r == 0:
@@ -333,15 +328,14 @@ def tile_knnxlmultiheadsattention_pb_s_kernel(tc, q, qkv, kv_external, gate, Wo,
             for vc, vg, lo, hi in VREGS.get(r, ()):
                 regroup_values(nc.vector.tensor_copy, vc, vg, lo, hi)
             if r > 0:
-                if r == 7:
-                    quantise_values(PAIRS - 1)
-                quantise_e(r - 1, 0, PASSES)
-                if r % 2 == 1 and r < last:
-                    quantise_values(c)
                 if r == last:
+                    quantise_values(PAIRS - 1)
                     w_codes = keep.tile([P, PASSES * P], U32, align_bytes=64)
                     w_scales = keep.tile([P, PASSES * P], U8, align_bytes=64)
                     nc.vector.quantize_mx(out=w_codes[:].bitcast(FP8X4), scales=w_scales[:], in_=w_grp[:])
+                quantise_e(r - 1, 0, PASSES)
+                if r % 2 == 1 and r < last:
+                    quantise_values(c)
                 if is_head(r - 2):
                     fuse(r - 2)
                 if r == 6:
@@ -366,21 +360,22 @@ def tile_knnxlmultiheadsattention_pb_s_kernel(tc, q, qkv, kv_external, gate, Wo,
             )
 
         weighted_values(last - 1)
-        keep_e(nc.vector.tensor_copy, last, 0, 1)
+        keep_e(nc.scalar.copy, last, 0, 1)
         keep_e(nc.scalar.copy, last, 1, 1)
+        regroup_words(nc.scalar.copy, m_grp[0][:], m0_ps[:])
         scale_sum(last)
         gate_local(last)
-        quantise_merged(0)
         quantise_e(last, 0, 1)
         invert_sums(last // 2)
         quantise_e(last, 1, 1)
-        fuse(last - 1)
         weighted_values(last)
-        out_ps = psum.tile([P, P], F32, tag="s", bufs=4)
-        project(0)
+        fuse(last - 1)
         fuse(last)
+        quantise_merged(0)
         m1_ps = psum.tile([P, 2, P], F32, tag="turned", bufs=3)
         turn_words(m1_ps, merged[:], 2, 2)
+        out_ps = psum.tile([P, P], F32, tag="s", bufs=4)
+        project(0)
         regroup_words(nc.vector.tensor_copy, m_grp[1][:], m1_ps[:])
         quantise_merged(1)
         project(1)

@@ -24,7 +24,6 @@ PASSES = 2
 PACK = 4
 PAIR_COLS = 2 * D
 PAIRS = H // 2
-SHARE_COLS = 64
 SCALE = D ** -0.5
 
 FLOPS = 2 * H * S * KEYS * D * 2 + 2 * S * HD * P
@@ -87,7 +86,7 @@ def tile_knnxlmultiheadsattention_pb_s_kernel(tc, q, qkv, kv_external, gate, Wo,
         s_ps, nb, e_sb, rs, dn, eT_ps, eT_grp, e_codes, e_scales, cf, pv_ps, kT_ps = (
             {}, {}, {}, {}, {}, {}, {}, {}, {}, {}, {}, {}
         )
-        v_grp, v_codes, v_scales, mx_both = {}, {}, {}, {}
+        v_grp, v_codes, v_scales, mx_both, pv_sb = {}, {}, {}, {}, {}
         qT = keep.tile([P, H, S], BF16)
         kT = keep.tile([P, H, KEYS], BF16)
         den = keep.tile([P, 2 * H], F32)
@@ -236,16 +235,14 @@ def tile_knnxlmultiheadsattention_pb_s_kernel(tc, q, qkv, kv_external, gate, Wo,
                 in_=v_sb[c][:, g * PACK : (g + 1) * PACK, lo:hi].rearrange("p t (c i) -> p c t i", i=4),
             )
 
-        def regroup_share(c, g, share):
-            cols = slice(share * SHARE_COLS, (share + 1) * SHARE_COLS)
-            nc.gpsimd.tensor_scalar(
-                out=v_grp[c][:, g, cols, :].rearrange("p (c i) t -> p c t i", i=4),
-                in0=v_sb[c][:, g * PACK : (g + 1) * PACK, cols].rearrange("p t (c i) -> p c t i", i=4),
-                scalar1=1.0,
-                scalar2=0.0,
-                op0=ALU.mult,
-                op1=ALU.add,
+        def fuse_on_scalar(h):
+            pv_sb[h] = work.tile([P, D], F32, name="pv_sb", tag="pv_sb")
+            nc.scalar.activation(
+                out=pv_sb[h][:], in_=pv_ps[h][:], func=ACT.Copy, scale=cf[h // 2][:, h % 2 : h % 2 + 1]
             )
+
+        def add_local(h):
+            nc.gpsimd.tensor_tensor(out=merged[:, h * D : (h + 1) * D], in0=pv_sb[h][:], in1=qg[:, h, :], op=ALU.add)
 
         def quantise_values(c):
             v_codes[c] = keep.tile([P, PASSES, PAIR_COLS], U32, name="v_codes%d" % c, align_bytes=64)
@@ -273,14 +270,13 @@ def tile_knnxlmultiheadsattention_pb_s_kernel(tc, q, qkv, kv_external, gate, Wo,
         keep_keys(nc.scalar.copy, 2)
         scores(1)
         row_max(1)
-        negate_max(1)
         turn_keys(3)
         turn_q(nc.vector.tensor_copy, 4, H)
+        negate_max(1)
         regroup_values(nc.vector.tensor_copy, 0, 0, 0, PAIR_COLS)
         regroup_values(nc.vector.tensor_copy, 0, 1, 0, PAIR_COLS)
 
-        VREGS = {1:[[1,0,0,256]],2:[[1,1,128,256]],3:[[2,0,0,256]],6:[[3,1,0,256]]}
-        SHARES = {1:[[1,1,0],[1,1,1]],3:[[2,1,0],[2,1,1]],4:[[2,1,2],[2,1,3]],5:[[3,0,0],[3,0,1],[3,0,2],[3,0,3]]}
+        VREGS = {1:[[1,0,0,256]],2:[[1,1,0,256]],3:[[2,0,0,256]],4:[[2,1,0,256]],5:[[3,0,0,256]],6:[[3,1,0,256]]}
         for r in range(H):
             exponentials(r, 0)
             if r == last:
@@ -292,6 +288,8 @@ def tile_knnxlmultiheadsattention_pb_s_kernel(tc, q, qkv, kv_external, gate, Wo,
                 turn_e(r, 0, PASSES, "turned", 3)
             else:
                 turn_e(r, 1, 1, "s", 4)
+            if 0 <= r - 3 < H // 2:
+                fuse_on_scalar(r - 3)
             if is_head(r - 2):
                 weighted_values(r - 2)
             if is_head(r - 1):
@@ -315,8 +313,6 @@ def tile_knnxlmultiheadsattention_pb_s_kernel(tc, q, qkv, kv_external, gate, Wo,
                 scale_sum(r - 1)
                 if r % 2 == 0:
                     invert_sums(r // 2 - 1)
-            if is_head(r + 2):
-                negate_max(r + 2)
             if r == 0:
                 nc.vector.reciprocal(out=g_sb[:], in_=den[:, 0:H])
             if is_head(r + 4):
@@ -327,6 +323,8 @@ def tile_knnxlmultiheadsattention_pb_s_kernel(tc, q, qkv, kv_external, gate, Wo,
             c = r // 2
             for vc, vg, lo, hi in VREGS.get(r, ()):
                 regroup_values(nc.vector.tensor_copy, vc, vg, lo, hi)
+            if is_head(r + 2):
+                negate_max(r + 2)
             if r > 0:
                 if r == last:
                     quantise_values(PAIRS - 1)
@@ -336,14 +334,14 @@ def tile_knnxlmultiheadsattention_pb_s_kernel(tc, q, qkv, kv_external, gate, Wo,
                 quantise_e(r - 1, 0, PASSES)
                 if r % 2 == 1 and r < last:
                     quantise_values(c)
-                if is_head(r - 2):
+                if H // 2 <= r - 2:
                     fuse(r - 2)
+                gate_local(r - 1)
+                if 0 <= r - 3 < H // 2:
+                    add_local(r - 3)
                 if r == 6:
                     m0_ps = psum.tile([P, 2, P], F32, tag="turned", bufs=3)
                     turn_words(m0_ps, merged[:], 0, 2)
-                gate_local(r - 1)
-                for gc, gg, gs in SHARES.get(r, ()):
-                    regroup_share(gc, gg, gs)
 
         def quantise_merged(g):
             nc.vector.quantize_mx(out=m_codes[g][:].bitcast(FP8X4), scales=m_scales[g][:], in_=m_grp[g][:])

@@ -94,10 +94,13 @@ def tile_knnxlmultiheadsattention_pb_s_kernel(tc, q, qkv, kv_external, gate, Wo,
         qg = keep.tile([P, H, D], F32)
         merged = keep.tile([P, HD], BF16)
 
-        def turn_q(copy, lo, hi):
+        def turn_q(lo, hi):
             q_ps = psum.tile([P, H, P], BF16, tag="turned", bufs=3)
             for h in range(lo, hi):
                 nc.tensor.transpose(q_ps[:, h, :], q_sb[:, h, :], ident_bf[:])
+            return q_ps
+
+        def keep_q(copy, lo, hi, q_ps):
             copy(out=qT[:, lo:hi, :].bitcast(F32), in_=q_ps[:, lo:hi, :].bitcast(F32))
 
         def turn_first_keys(copy, w):
@@ -229,10 +232,10 @@ def tile_knnxlmultiheadsattention_pb_s_kernel(tc, q, qkv, kv_external, gate, Wo,
         for c in range(PAIRS):
             v_grp[c] = keep.tile([P, PASSES, PAIR_COLS, PACK], BF16, name="v_grp%d" % c, align_bytes=64)
 
-        def regroup_values(copy, c, g, lo, hi):
-            copy(
-                out=v_grp[c][:, g, lo:hi, :].rearrange("p (c i) t -> p c t i", i=4),
-                in_=v_sb[c][:, g * PACK : (g + 1) * PACK, lo:hi].rearrange("p t (c i) -> p c t i", i=4),
+        def regroup_values(c, g):
+            nc.vector.tensor_copy(
+                out=v_grp[c][:, g].rearrange("p (c i) t -> p c t i", i=4),
+                in_=v_sb[c][:, g * PACK : (g + 1) * PACK, :].rearrange("p t (c i) -> p c t i", i=4),
             )
 
         def fuse_on_scalar(h):
@@ -258,25 +261,24 @@ def tile_knnxlmultiheadsattention_pb_s_kernel(tc, q, qkv, kv_external, gate, Wo,
 
         last = H - 1
         turn_first_keys(nc.vector.tensor_copy, 0)
-        turn_q(nc.scalar.copy, 0, 2)
+        keep_q(nc.scalar.copy, 0, 2, turn_q(0, 2))
         turn_first_keys(nc.scalar.copy, 1)
         turn_first_keys(nc.vector.tensor_copy, 2)
         turn_first_keys(nc.vector.tensor_copy, 3)
         scores(0)
         row_max(0)
         negate_max(0)
-        turn_q(nc.scalar.copy, 2, 4)
+        keep_q(nc.scalar.copy, 2, 4, turn_q(2, 4))
         turn_keys(2)
         keep_keys(nc.scalar.copy, 2)
         scores(1)
         row_max(1)
         turn_keys(3)
-        turn_q(nc.vector.tensor_copy, 4, H)
+        q_ps = turn_q(4, H)
         negate_max(1)
-        regroup_values(nc.vector.tensor_copy, 0, 0, 0, PAIR_COLS)
-        regroup_values(nc.vector.tensor_copy, 0, 1, 0, PAIR_COLS)
+        regroup_values(0, 0)
+        regroup_values(0, 1)
 
-        VREGS = {1:[[1,0,0,256]],2:[[1,1,0,256]],3:[[2,0,0,256]],4:[[2,1,0,256]],5:[[3,0,0,256]],6:[[3,1,0,256]]}
         for r in range(H):
             exponentials(r, 0)
             if r == last:
@@ -297,6 +299,7 @@ def tile_knnxlmultiheadsattention_pb_s_kernel(tc, q, qkv, kv_external, gate, Wo,
             if is_head(r + 3):
                 keep_keys(nc.scalar.copy, r + 3)
             if r == 0:
+                keep_q(nc.scalar.copy, 4, H, q_ps)
                 nc.scalar.activation(out=den[:, 0:H], in_=gate_sb[:], func=ACT.Exp, scale=-1.0)
                 nc.scalar.activation(out=den[:, H : 2 * H], in_=gate_sb[:], func=ACT.Exp, scale=1.0)
             if r == 5:
@@ -305,6 +308,8 @@ def tile_knnxlmultiheadsattention_pb_s_kernel(tc, q, qkv, kv_external, gate, Wo,
                 m_grp = [keep.tile([P, BANK], BF16, name="m_grp%d" % g, align_bytes=64) for g in range(PASSES)]
                 m_codes = [keep.tile([P, P], U32, name="m_codes%d" % g, align_bytes=64) for g in range(PASSES)]
                 m_scales = [keep.tile([P, P], U8, name="m_scales%d" % g, align_bytes=64) for g in range(PASSES)]
+            if r % 2 == 1 and r < last:
+                quantise_values(r // 2)
             if is_head(r + 2):
                 row_max(r + 2)
             if r == 0:
@@ -320,9 +325,8 @@ def tile_knnxlmultiheadsattention_pb_s_kernel(tc, q, qkv, kv_external, gate, Wo,
             if r == 4:
                 w_ps = psum.tile([P, 2 * PASSES, P], F32, tag="turned", bufs=3)
                 turn_words(w_ps, wo_sb[:], 0, 2 * PASSES)
-            c = r // 2
-            for vc, vg, lo, hi in VREGS.get(r, ()):
-                regroup_values(nc.vector.tensor_copy, vc, vg, lo, hi)
+            if 0 < r < last:
+                regroup_values((r + 1) // 2, (r + 1) % 2)
             if is_head(r + 2):
                 negate_max(r + 2)
             if r > 0:
@@ -332,8 +336,6 @@ def tile_knnxlmultiheadsattention_pb_s_kernel(tc, q, qkv, kv_external, gate, Wo,
                     w_scales = keep.tile([P, PASSES * P], U8, align_bytes=64)
                     nc.vector.quantize_mx(out=w_codes[:].bitcast(FP8X4), scales=w_scales[:], in_=w_grp[:])
                 quantise_e(r - 1, 0, PASSES)
-                if r % 2 == 1 and r < last:
-                    quantise_values(c)
                 if H // 2 <= r - 2:
                     fuse(r - 2)
                 gate_local(r - 1)

from contextlib import ExitStack

import concourse.mybir as mybir
from concourse.masks import make_identity

BF16 = mybir.dt.bfloat16
F32 = mybir.dt.float32
U32 = mybir.dt.uint32
U8 = mybir.dt.uint8
FP8X4 = mybir.dt.float8_e4m3fn_x4
ACT = mybir.ActivationFunctionType
ALU = mybir.AluOpType
AX = mybir.AxisListType

P = 128
H = 8
D = 128
S = 128
T = 8
HD = H * D
KEYS = S * T
BANK = 512
PASSES = 2
PACK = 4
PAIR_COLS = 2 * D
PAIRS = H // 2
SCALE = D ** -0.5

FLOPS = 2 * H * S * KEYS * D * 2 + 2 * S * HD * P


def tile_knnxlmultiheadsattention_pb_s_kernel(tc, q, qkv, kv_external, gate, Wo, bo, out):
    nc = tc.nc
    kv = kv_external.rearrange("b j t c n -> (b j) t c n")
    q_rows = q.rearrange("b h i d -> i (b h) d")

    with ExitStack() as ctx:
        keep = ctx.enter_context(tc.tile_pool(name="keep", bufs=1))
        work = ctx.enter_context(tc.tile_pool(name="work", bufs=3))
        psum = ctx.enter_context(tc.psum_pool(name="psum", bufs=1))
        ctx.enter_context(tc.manual_schedule())

        zero = keep.tile([P, 1], F32)
        nc.vector.memset(zero[:], 0.0)
        one = keep.tile([P, 1], F32)
        nc.scalar.activation(out=one[:], in_=zero[:], func=ACT.Exp)
        ident_bf = keep.tile([P, P], BF16)
        make_identity(nc, ident_bf[:])
        ident_f32 = keep.tile([P, P], F32)
        make_identity(nc, ident_f32[:])

        k_sb = [keep.tile([P, T, PAIR_COLS], BF16, name="k_sb%d" % c) for c in range(PAIRS)]
        v_sb = [keep.tile([P, T, PAIR_COLS], BF16, name="v_sb%d" % c) for c in range(PAIRS)]
        q_sb = keep.tile([P, H, D], BF16)
        gate_sb = keep.tile([P, H], BF16)
        qkv_sb = keep.tile([P, H, D], BF16)
        wo_sb = keep.tile([P, HD], BF16)
        bo_sb = keep.tile([P, P], BF16)

        def load_keys(c, lo, hi):
            nc.sync.dma_start(out=k_sb[c][:, lo:hi, :], in_=kv[:, lo:hi, 0, c * PAIR_COLS : (c + 1) * PAIR_COLS])

        def load_values(c, lo, hi):
            nc.sync.dma_start(out=v_sb[c][:, lo:hi, :], in_=kv[:, lo:hi, 1, c * PAIR_COLS : (c + 1) * PAIR_COLS])

        load_keys(0, 0, 2)
        nc.sync.dma_start(out=q_sb[:, 0:2, :], in_=q_rows[:, 0:2, :])
        load_keys(0, 2, 4)
        load_keys(0, 4, 6)
        load_keys(0, 6, 8)
        nc.sync.dma_start(out=q_sb[:, 2:4, :], in_=q_rows[:, 2:4, :])
        load_keys(1, 0, T)
        nc.sync.dma_start(out=q_sb[:, 4:H, :], in_=q_rows[:, 4:H, :])
        load_values(0, 0, PACK)
        load_values(0, PACK, T)
        nc.sync.dma_start(out=gate_sb[:], in_=gate.rearrange("h a b -> (h a b)").partition_broadcast(P))
        load_keys(2, 0, T)
        load_values(1, 0, T)
        nc.sync.dma_start(out=qkv_sb[:], in_=qkv.rearrange("b h i d -> i (b h) d"))
        load_keys(3, 0, T)
        load_values(2, 0, T)
        load_values(3, 0, T)
        nc.sync.dma_start(out=wo_sb[:], in_=Wo)
        nc.sync.dma_start(out=bo_sb[:], in_=bo.partition_broadcast(P))

        s_ps, nb, e_sb, rs, dn, eT_ps, eT_grp, e_codes, e_scales, cf, pv_ps, kT_ps = (
            {}, {}, {}, {}, {}, {}, {}, {}, {}, {}, {}, {}
        )
        v_grp, v_codes, v_scales, mx_both, pv_sb = {}, {}, {}, {}, {}
        qT = keep.tile([P, H, S], BF16)
        kT = keep.tile([P, H, KEYS], BF16)
        den = keep.tile([P, 2 * H], F32)
        g_sb = keep.tile([P, H], F32)
        qg = keep.tile([P, H, D], F32)
        merged = keep.tile([P, HD], BF16)

        def turn_q(lo, hi):
            q_ps = psum.tile([P, H, P], BF16, tag="turned", bufs=3)
            for h in range(lo, hi):
                nc.tensor.transpose(q_ps[:, h, :], q_sb[:, h, :], ident_bf[:])
            return q_ps

        def keep_q(copy, lo, hi, q_ps):
            copy(out=qT[:, lo:hi, :].bitcast(F32), in_=q_ps[:, lo:hi, :].bitcast(F32))

        def turn_first_keys(copy, w):
            k_ps = psum.tile([P, 2, 2, P], BF16, tag="turned", bufs=3)
            for h in range(2):
                for t in range(2):
                    nc.tensor.transpose(k_ps[:, h, t, :], k_sb[0][:, 2 * w + t, h * D : (h + 1) * D], ident_bf[:])
            copy(
                out=kT[:, 0:2, 2 * w * P : (2 * w + 2) * P].bitcast(F32),
                in_=k_ps[:].rearrange("p h t r -> p h (t r)").bitcast(F32),
            )

        def turn_keys(h):
            kT_ps[h] = psum.tile([P, T, P], BF16, name="kT_ps", tag="turned", bufs=3)
            for t in range(T):
                rows = k_sb[h // 2][:, t, (h % 2) * D : (h % 2 + 1) * D]
                nc.tensor.transpose(kT_ps[h][:, t, :], rows, ident_bf[:])

        def keep_keys(copy, h):
            copy(out=kT[:, h, :].bitcast(F32), in_=kT_ps[h][:].rearrange("p t r -> p (t r)").bitcast(F32))

        def turn_words(turned, rows, first, count):
            words = rows.bitcast(F32)
            for b in range(count):
                nc.tensor.transpose(turned[:, b, :], words[:, (first + b) * P : (first + b + 1) * P], ident_f32[:])

        def regroup_words(copy, grouped, turned):
            copy(
                out=grouped.bitcast(F32).rearrange("p (g r u) -> p g r u", r=P, u=2),
                in_=turned.rearrange("p (g u) r -> p g r u", u=2),
            )

        def scores(h):
            s_ps[h] = []
            for g in range(PASSES):
                s_g = psum.tile([P, BANK], F32, tag="s", bufs=4)
                nc.tensor.matmul(
                    s_g[:], lhsT=qT[:, h, :], rhs=kT[:, h, g * BANK : (g + 1) * BANK], start=True, stop=True
                )
                s_ps[h].append(s_g)

        def row_max(h):
            mx = work.tile([P, PASSES], F32, tag="mx")
            for g in range(PASSES):
                nc.vector.reduce_max(out=mx[:, g : g + 1], in_=s_ps[h][g][:], axis=AX.X)
            mx_both[h] = mx

        def negate_max(h):
            nb[h] = work.tile([P, 1], F32, name="nb", tag="nb")
            nc.vector.tensor_scalar(
                out=nb[h][:], in0=mx_both[h][:, 0:1], scalar1=mx_both[h][:, 1:2], scalar2=-SCALE,
                op0=ALU.max, op1=ALU.mult,
            )

        def exponentials(h, g):
            if g == 0:
                e_sb[h] = work.tile([P, KEYS], BF16, name="e_sb", tag="e_sb")
                rs[h] = work.tile([P, PASSES], F32, name="rs", tag="rs")
            nc.scalar.activation(
                out=e_sb[h][:, g * BANK : (g + 1) * BANK].rearrange("p (u j e) -> p u j e", u=2, e=2),
                in_=s_ps[h][g][:].rearrange("p (u e j) -> p u j e", u=2, e=2),
                func=ACT.Exp,
                bias=nb[h][:, 0:1],
                scale=SCALE,
                accum_out=rs[h][:, g : g + 1],
            )

        def scale_sum(h):
            if h % 2 == 0:
                dn[h // 2] = work.tile([P, 2], F32, name="dn", tag="dn")
            nc.gpsimd.tensor_scalar(
                out=dn[h // 2][:, h % 2 : h % 2 + 1], in0=rs[h][:, 0:1], scalar1=rs[h][:, 1:2], scalar2=den[:, H + h : H + h + 1],
                op0=ALU.add, op1=ALU.mult,
            )

        def gate_local(h):
            nc.gpsimd.tensor_scalar(
                out=qg[:, h, :], in0=qkv_sb[:, h, :], scalar1=g_sb[:, h : h + 1], scalar2=0.0,
                op0=ALU.mult, op1=ALU.add,
            )

        def turn_e(h, g, count, tag, bufs):
            eT_ps[h, g] = psum.tile([P, 2 * count, P], F32, name="eT_ps", tag=tag, bufs=bufs)
            turn_words(eT_ps[h, g], e_sb[h][:], 2 * g, 2 * count)

        def keep_e(copy, h, g, count):
            if g == 0:
                eT_grp[h] = work.tile([P, KEYS], BF16, name="eT_grp", tag="eT_grp", align_bytes=64)
            regroup_words(copy, eT_grp[h][:, g * BANK : (g + count) * BANK], eT_ps[h, g][:])

        def quantise_e(h, g, count):
            if g == 0:
                e_codes[h] = work.tile([P, PASSES * P], U32, name="e_codes", tag="e_codes", align_bytes=64)
                e_scales[h] = work.tile([P, PASSES * P], U8, name="e_scales", tag="e_scales", align_bytes=64)
            words = slice(g * P, (g + count) * P)
            nc.vector.quantize_mx(
                out=e_codes[h][:, words].bitcast(FP8X4),
                scales=e_scales[h][:, words],
                in_=eT_grp[h][:, g * BANK : (g + count) * BANK],
            )

        def invert_sums(c):
            cf[c] = work.tile([P, 2], F32, name="cf", tag="cf")
            nc.vector.reciprocal(out=cf[c][:], in_=dn[c][:])

        def weighted_values(h):
            if h < H - 1:
                pv_ps[h] = psum.tile([P, D], F32, name="pv_ps", tag="pv", bufs=1)
            else:
                pv_ps[h] = psum.tile([P, D], F32, name="pv_ps", tag="s", bufs=4)
            cols = slice((h % 2) * D, (h % 2 + 1) * D)
            for g in range(PASSES):
                nc.tensor.matmul_mx(
                    out=pv_ps[h][:],
                    lhsT=e_codes[h][:, g * P : (g + 1) * P].bitcast(FP8X4),
                    lhsT_scale=e_scales[h][:, g * P : (g + 1) * P],
                    rhs=v_codes[h // 2][:, g, cols].bitcast(FP8X4),
                    rhs_scale=v_scales[h // 2][:, g, cols],
                    start=(g == 0),
                    stop=(g == PASSES - 1),
                )

        def fuse(h):
            nc.vector.scalar_tensor_tensor(
                out=merged[:, h * D : (h + 1) * D], in0=pv_ps[h][:], scalar=cf[h // 2][:, h % 2 : h % 2 + 1], in1=qg[:, h, :],
                op0=ALU.mult, op1=ALU.add,
            )

        for c in range(PAIRS):
            v_grp[c] = keep.tile([P, PASSES, PAIR_COLS, PACK], BF16, name="v_grp%d" % c, align_bytes=64)

        def regroup_values(c, g):
            nc.vector.tensor_copy(
                out=v_grp[c][:, g].rearrange("p (c i) t -> p c t i", i=4),
                in_=v_sb[c][:, g * PACK : (g + 1) * PACK, :].rearrange("p t (c i) -> p c t i", i=4),
            )

        def fuse_on_scalar(h):
            pv_sb[h] = work.tile([P, D], F32, name="pv_sb", tag="pv_sb")
            nc.scalar.activation(
                out=pv_sb[h][:], in_=pv_ps[h][:], func=ACT.Copy, scale=cf[h // 2][:, h % 2 : h % 2 + 1]
            )

        def add_local(h):
            nc.gpsimd.tensor_tensor(out=merged[:, h * D : (h + 1) * D], in0=pv_sb[h][:], in1=qg[:, h, :], op=ALU.add)

        def quantise_values(c):
            v_codes[c] = keep.tile([P, PASSES, PAIR_COLS], U32, name="v_codes%d" % c, align_bytes=64)
            v_scales[c] = keep.tile([P, PASSES, PAIR_COLS], U8, name="v_scales%d" % c, align_bytes=64)
            nc.vector.quantize_mx(
                out=v_codes[c][:].rearrange("p g c -> p (g c)").bitcast(FP8X4),
                scales=v_scales[c][:].rearrange("p g c -> p (g c)"),
                in_=v_grp[c][:].rearrange("p g c t -> p (g c t)"),
            )

        def is_head(h):
            return 0 <= h < H

        last = H - 1
        turn_first_keys(nc.vector.tensor_copy, 0)
        keep_q(nc.scalar.copy, 0, 2, turn_q(0, 2))
        turn_first_keys(nc.scalar.copy, 1)
        turn_first_keys(nc.vector.tensor_copy, 2)
        turn_first_keys(nc.vector.tensor_copy, 3)
        scores(0)
        row_max(0)
        negate_max(0)
        keep_q(nc.scalar.copy, 2, 4, turn_q(2, 4))
        turn_keys(2)
        keep_keys(nc.scalar.copy, 2)
        scores(1)
        row_max(1)
        turn_keys(3)
        q_ps = turn_q(4, H)
        negate_max(1)
        regroup_values(0, 0)
        regroup_values(0, 1)

        for r in range(H):
            exponentials(r, 0)
            if r == last:
                turn_e(r, 0, 1, "s", 4)
            exponentials(r, 1)
            if is_head(r + 2):
                scores(r + 2)
            if r < last:
                turn_e(r, 0, PASSES, "turned", 3)
            else:
                turn_e(r, 1, 1, "s", 4)
            if 0 <= r - 3 < H // 2:
                fuse_on_scalar(r - 3)
            if is_head(r - 2):
                weighted_values(r - 2)
            if is_head(r - 1):
                keep_e(nc.scalar.copy, r - 1, 0, PASSES)
            if is_head(r + 3):
                keep_keys(nc.scalar.copy, r + 3)
            if r == 0:
                keep_q(nc.scalar.copy, 4, H, q_ps)
                nc.scalar.activation(out=den[:, 0:H], in_=gate_sb[:], func=ACT.Exp, scale=-1.0)
                nc.scalar.activation(out=den[:, H : 2 * H], in_=gate_sb[:], func=ACT.Exp, scale=1.0)
            if r == 5:
                w_grp = keep.tile([P, HD], BF16, align_bytes=64)
                regroup_words(nc.scalar.copy, w_grp[:], w_ps[:])
                m_grp = [keep.tile([P, BANK], BF16, name="m_grp%d" % g, align_bytes=64) for g in range(PASSES)]
                m_codes = [keep.tile([P, P], U32, name="m_codes%d" % g, align_bytes=64) for g in range(PASSES)]
                m_scales = [keep.tile([P, P], U8, name="m_scales%d" % g, align_bytes=64) for g in range(PASSES)]
            if r % 2 == 1 and r < last:
                quantise_values(r // 2)
            if is_head(r + 2):
                row_max(r + 2)
            if r == 0:
                nc.vector.tensor_scalar_add(out=den[:], in0=den[:], scalar1=1.0)
            if r > 0:
                scale_sum(r - 1)
                if r % 2 == 0:
                    invert_sums(r // 2 - 1)
            if r == 0:
                nc.vector.reciprocal(out=g_sb[:], in_=den[:, 0:H])
            if is_head(r + 4):
                turn_keys(r + 4)
            if r == 4:
                w_ps = psum.tile([P, 2 * PASSES, P], F32, tag="turned", bufs=3)
                turn_words(w_ps, wo_sb[:], 0, 2 * PASSES)
            if 0 < r < last:
                regroup_values((r + 1) // 2, (r + 1) % 2)
            if is_head(r + 2):
                negate_max(r + 2)
            if r > 0:
                if r == last:
                    quantise_values(PAIRS - 1)
                    w_codes = keep.tile([P, PASSES * P], U32, align_bytes=64)
                    w_scales = keep.tile([P, PASSES * P], U8, align_bytes=64)
                    nc.vector.quantize_mx(out=w_codes[:].bitcast(FP8X4), scales=w_scales[:], in_=w_grp[:])
                quantise_e(r - 1, 0, PASSES)
                if H // 2 <= r - 2:
                    fuse(r - 2)
                gate_local(r - 1)
                if 0 <= r - 3 < H // 2:
                    add_local(r - 3)
                if r == 6:
                    m0_ps = psum.tile([P, 2, P], F32, tag="turned", bufs=3)
                    turn_words(m0_ps, merged[:], 0, 2)

        def quantise_merged(g):
            nc.vector.quantize_mx(out=m_codes[g][:].bitcast(FP8X4), scales=m_scales[g][:], in_=m_grp[g][:])

        def project(g):
            nc.tensor.matmul_mx(
                out=out_ps[:],
                lhsT=m_codes[g][:].bitcast(FP8X4),
                lhsT_scale=m_scales[g][:],
                rhs=w_codes[:, g * P : (g + 1) * P].bitcast(FP8X4),
                rhs_scale=w_scales[:, g * P : (g + 1) * P],
                start=(g == 0),
                stop=(g == PASSES - 1),
            )

        weighted_values(last - 1)
        keep_e(nc.scalar.copy, last, 0, 1)
        keep_e(nc.scalar.copy, last, 1, 1)
        regroup_words(nc.scalar.copy, m_grp[0][:], m0_ps[:])
        scale_sum(last)
        gate_local(last)
        quantise_e(last, 0, 1)
        invert_sums(last // 2)
        quantise_e(last, 1, 1)
        weighted_values(last)
        fuse(last - 1)
        fuse(last)
        quantise_merged(0)
        m1_ps = psum.tile([P, 2, P], F32, tag="turned", bufs=3)
        turn_words(m1_ps, merged[:], 2, 2)
        out_ps = psum.tile([P, P], F32, tag="s", bufs=4)
        project(0)
        regroup_words(nc.vector.tensor_copy, m_grp[1][:], m1_ps[:])
        quantise_merged(1)
        project(1)
        out_sb = keep.tile([P, P], F32)
        nc.vector.tensor_tensor(out=out_sb[:], in0=out_ps[:], in1=bo_sb[:], op=ALU.add)
        nc.sync.dma_start(out=out.rearrange("b i e -> (b i) e"), in_=out_sb[:])
